import numpy as np
import ml_dtypes


def mxq(x, axis, fmt="e4m3"):
    dtype, down = {"e4m3": (ml_dtypes.float8_e4m3fn, 7), "e5m2": (ml_dtypes.float8_e5m2, 14)}[fmt]
    v = np.moveaxis(np.asarray(x, np.float32).astype(ml_dtypes.bfloat16).astype(np.float64), axis, -1)
    blocks = v.reshape(v.shape[:-1] + (-1, 32))
    amax = np.abs(blocks).max(-1, keepdims=True)
    byte = np.maximum(np.where(amax > 0, np.frexp(amax)[1] - 1 + 127, 0) - down, 1)
    scale = np.exp2(byte - 127.0)
    codes = (blocks / scale).astype(np.float32).astype(dtype).astype(np.float64)
    return np.moveaxis((codes * scale).reshape(v.shape), -1, axis)


WIDE = False


def mx_kscale(k):
    if not WIDE:
        return np.ones(k)
    levels = np.array([10, -10, 5, -5, 0])
    a = np.random.permutation(np.resize(levels, k // 512 * 4)).reshape(k // 512, 4)
    idx = np.arange(k)
    return np.exp2(a[idx // 512, idx % 128 // 32])


BF16 = ml_dtypes.bfloat16


def bf(x):
    return np.asarray(x, np.float32).astype(BF16)


def f64(x):
    return np.asarray(x).astype(np.float64)


B, T, E, V, NH, C = 4, 1024, 256, 1024, 2, 512
KD, HD = E // NH, V // NH


def make_decay_mask():
    gamma = 1.0 - np.exp2(-5.0 - np.arange(NH))
    n = np.arange(T)
    diff = n[:, None] - n[None, :]
    tri = diff >= 0
    expnt = np.where(tri, diff, 0)
    dm = np.where(tri[None], gamma[:, None, None] ** expnt[None], 0.0)
    dm = dm / np.sqrt(dm.sum(-1, keepdims=True))
    return dm[None]


def setup_inputs():
    t = mx_kscale(T)
    t = t / t.max()
    return {"qr": bf(np.random.standard_normal((B, NH, T, KD))),
            "kr": bf(np.random.standard_normal((B, NH, T, KD)) * 2.0 * KD ** -0.5 * t[:, None]),
            "v": bf(np.random.standard_normal((B, NH, T, HD)) / t[:, None]),
            "decay_mask": bf(make_decay_mask())}


def reference(qr, kr, v, decay_mask):
    qr, kr, dm = f64(qr), f64(kr), f64(decay_mask)
    vq = mxq(f64(v), 2, "e4m3")
    outs = []
    for i in range(T // C):
        lo, hi = i * C, (i + 1) * C
        ret = (qr[:, :, lo:hi] @ kr[:, :, :hi].transpose(0, 1, 3, 2)) * dm[:, :, lo:hi, :hi]
        denom = np.maximum(np.abs(ret.sum(-1, keepdims=True)), 1.0)
        ret = ret / denom
        outs.append(mxq(ret, 3, "e4m3") @ vq[:, :, :hi])
    return np.concatenate(outs, axis=2)

@@ -1,0 +1,216 @@
+from contextlib import ExitStack
+
+import concourse.mybir as mybir
+from concourse.masks import make_identity
+
+F32 = mybir.dt.float32
+BF16 = mybir.dt.bfloat16
+U32 = mybir.dt.uint32
+U8 = mybir.dt.uint8
+FP8X4 = mybir.dt.float8_e4m3fn_x4
+MULT = mybir.AluOpType.mult
+MAX = mybir.AluOpType.max
+COPY = mybir.ActivationFunctionType.Copy
+
+B, NH, T, KD, HD = 4, 2, 1024, 128, 512
+P = 128
+PACK = 4
+K_PASS = P * PACK
+TB = T // P
+BLOCKS_PER_CHUNK = K_PASS // P
+N_CHUNKS = T // K_PASS
+
+FLOPS = 2 * B * NH * sum(K_PASS * K_PASS * (c + 1) for c in range(N_CHUNKS)) * (KD + HD)
+
+
+def tile_nucleusxmultiscaleretention_pb_t_kernel(tc, qr, kr, v, decay_mask, out):
+    nc = tc.nc
+    heads = [(b, h) for b in range(B) for h in range(NH)]
+
+    with ExitStack() as ctx:
+        const = ctx.enter_context(tc.tile_pool(name="const", bufs=1))
+        inputs = ctx.enter_context(tc.tile_pool(name="inputs", bufs=1))
+        per_head = ctx.enter_context(tc.tile_pool(name="per_head", bufs=2))
+        stream = ctx.enter_context(tc.tile_pool(name="stream", bufs=3))
+        results = ctx.enter_context(tc.tile_pool(name="results", bufs=4))
+        psum_scores = ctx.enter_context(tc.psum_pool(name="psum_scores", bufs=3))
+        psum_turned = ctx.enter_context(tc.psum_pool(name="psum_turned", bufs=3))
+        psum_out = ctx.enter_context(tc.psum_pool(name="psum_out", bufs=2))
+
+        q_rows, k_rows, v_rows, mask_tiles = [], [], [], {}
+        for i, (b, h) in enumerate(heads):
+            q_sb = inputs.tile([P, TB, KD], BF16, name="q_sb%d" % i)
+            nc.sync.dma_start(out=q_sb[:], in_=qr[b, h].rearrange("(n p) d -> p n d", p=P))
+            k_sb = inputs.tile([P, TB, KD], BF16, name="k_sb%d" % i)
+            nc.sync.dma_start(out=k_sb[:], in_=kr[b, h].rearrange("(n p) d -> p n d", p=P))
+            if b == 0:
+                for c in range(N_CHUNKS):
+                    keys = K_PASS * (c + 1)
+                    mask = inputs.tile(
+                        [P, BLOCKS_PER_CHUNK, keys], BF16, name="mask%d_%d" % (h, c)
+                    )
+                    nc.sync.dma_start(
+                        out=mask[:],
+                        in_=decay_mask[0, h, c * K_PASS : (c + 1) * K_PASS, 0:keys].rearrange(
+                            "(n p) s -> p n s", p=P
+                        ),
+                    )
+                    mask_tiles[(h, c)] = mask
+            v_sb = inputs.tile([P, N_CHUNKS, PACK, HD], BF16, name="v_sb%d" % i)
+            nc.sync.dma_start(
+                out=v_sb[:].rearrange("p g (u e) n -> p (g u) (e n)", e=2),
+                in_=v[b, h].rearrange("(a p e) n -> p a (e n)", p=P, e=2),
+            )
+            q_rows.append(q_sb)
+            k_rows.append(k_sb)
+            v_rows.append(v_sb)
+
+        ident_bf = const.tile([P, P], BF16, name="ident_bf")
+        make_identity(nc, ident_bf[:])
+        ident_f32 = const.tile([P, P], F32, name="ident_f32")
+        make_identity(nc, ident_f32[:])
+
+        p_tiles = []
+        for half in range(2):
+            p_set = []
+            for tb in range(TB):
+                width = K_PASS * (tb // BLOCKS_PER_CHUNK + 1)
+                p_sb = const.tile([P, width], BF16, name="p_sb%d_%d" % (half, tb))
+                if (tb + 1) * P < width:
+                    nc.vector.memset(p_sb[:, (tb + 1) * P :], 0.0)
+                p_set.append(p_sb)
+            p_tiles.append(p_set)
+
+        handed_on = {}
+
+        def turn_rows(rows, tag):
+            turned_ps = psum_turned.tile([P, TB, P], BF16, tag="turned")
+            for n in range(TB):
+                nc.tensor.transpose(turned_ps[:, n, :], rows[:, n, :], ident_bf[:])
+            turned = per_head.tile([P, T], BF16, tag=tag, name=tag)
+            nc.scalar.copy(out=turned[:], in_=turned_ps[:].rearrange("d n t -> d (n t)"))
+            return turned
+
+        def start_head(i):
+            state = {"qT": turn_rows(q_rows[i], "qT"), "kT": turn_rows(k_rows[i], "kT")}
+            v_codes = per_head.tile([P, N_CHUNKS, HD], U32, tag="v_codes", align_bytes=64)
+            v_scales = per_head.tile([P, N_CHUNKS, HD], U8, tag="v_scales", align_bytes=64)
+            grouped = []
+            for g in range(N_CHUNKS):
+                v_grouped = per_head.tile([P, HD * PACK], BF16, tag="v_grouped", align_bytes=64)
+                nc.vector.tensor_copy(
+                    out=v_grouped[:].rearrange("p (c i j) -> p c j i", i=4, j=PACK),
+                    in_=v_rows[i][:, g].rearrange("p j (c i) -> p c j i", i=4),
+                )
+                grouped.append(v_grouped)
+            for g in range(N_CHUNKS):
+                nc.vector.quantize_mx(
+                    out=v_codes[:, g, :].bitcast(FP8X4),
+                    scales=v_scales[:, g, :],
+                    in_=grouped[g][:],
+                )
+            state["v_codes"] = v_codes
+            state["v_scales"] = v_scales
+            state["sums"] = per_head.tile([P, N_CHUNKS, TB], F32, tag="sums", name="sums")
+            state["r"] = []
+            handed_on[i] = state
+
+        def mask_scores(i, tb):
+            state = handed_on[i]
+            h = heads[i][1]
+            mask = mask_tiles[(h, tb // BLOCKS_PER_CHUNK)]
+            keys = (tb + 1) * P
+            r_sb = per_head.tile([P, keys], F32, tag="r%d" % tb, name="r%d" % tb)
+            for g in range(tb // BLOCKS_PER_CHUNK + 1):
+                lo = g * K_PASS
+                hi = min(keys, lo + K_PASS)
+                scores = psum_scores.tile([P, K_PASS], F32, tag="scores")
+                nc.tensor.matmul(
+                    scores[:, : hi - lo],
+                    lhsT=state["qT"][:, tb * P : (tb + 1) * P],
+                    rhs=state["kT"][:, lo:hi],
+                    start=True,
+                    stop=True,
+                )
+                nc.vector.scalar_tensor_tensor(
+                    out=r_sb[:, lo:hi],
+                    in0=scores[:, : hi - lo],
+                    scalar=1.0,
+                    in1=mask[:, tb % BLOCKS_PER_CHUNK, lo:hi],
+                    op0=MULT,
+                    op1=MULT,
+                    accum_out=state["sums"][:, g, tb : tb + 1],
+                )
+            state["r"].append(r_sb)
+
+        def invert_row_sums(i):
+            state = handed_on[i]
+            sums = state["sums"]
+            first = sums[:, 0, :]
+            late = slice(BLOCKS_PER_CHUNK, TB)
+            nc.vector.tensor_add(out=first[:, late], in0=first[:, late], in1=sums[:, 1, late])
+            clipped = per_head.tile([P, TB], F32, tag="clipped")
+            nc.vector.tensor_scalar_max(out=clipped[:], in0=first, scalar1=1.0)
+            denom = per_head.tile([P, TB], F32, tag="denom")
+            nc.vector.scalar_tensor_tensor(
+                out=denom[:], in0=first, scalar=-1.0, in1=clipped[:], op0=MULT, op1=MAX
+            )
+            inverse = per_head.tile([P, TB], F32, tag="inverse")
+            nc.vector.reciprocal(out=inverse[:], in_=denom[:])
+            state["inverse"] = inverse
+
+        def finish_block(i, tb):
+            state = handed_on[i]
+            b, h = heads[i]
+            keys = (tb + 1) * P
+            passes = tb // BLOCKS_PER_CHUNK + 1
+            p_sb = p_tiles[i % 2][tb]
+            r_sb = state["r"][tb]
+            scale = state["inverse"][:, tb : tb + 1]
+            if tb % 3 == 0:
+                nc.vector.tensor_scalar_mul(out=p_sb[:, :keys], in0=r_sb[:], scalar1=scale)
+            else:
+                nc.scalar.activation(out=p_sb[:, :keys], in_=r_sb[:], func=COPY, scale=scale)
+
+            words = p_sb[:].bitcast(F32)
+            turned = psum_turned.tile([P, passes, 2, P], F32, tag="turned")
+            for g in range(passes):
+                for u in range(2):
+                    w0 = (2 * g + u) * P
+                    nc.tensor.transpose(turned[:, g, u, :], words[:, w0 : w0 + P], ident_f32[:])
+            p_grouped = stream.tile([P, passes * K_PASS], BF16, tag="p_grouped", align_bytes=64)
+            nc.scalar.copy(
+                out=p_grouped[:].bitcast(F32).rearrange("p (g t u) -> p g t u", g=passes, u=2),
+                in_=turned[:].rearrange("p g u t -> p g t u"),
+            )
+            p_codes = stream.tile([P, passes * P], U32, tag="p_codes", align_bytes=64)
+            p_scales = stream.tile([P, passes * P], U8, tag="p_scales", align_bytes=64)
+            nc.vector.quantize_mx(
+                out=p_codes[:].bitcast(FP8X4), scales=p_scales[:], in_=p_grouped[:]
+            )
+
+            acc = psum_out.tile([P, HD], F32, tag="acc")
+            for g in range(passes):
+                nc.tensor.matmul_mx(
+                    out=acc[:],
+                    lhsT=p_codes[:, g * P : (g + 1) * P].bitcast(FP8X4),
+                    lhsT_scale=p_scales[:, g * P : (g + 1) * P],
+                    rhs=state["v_codes"][:, g, :].bitcast(FP8X4),
+                    rhs_scale=state["v_scales"][:, g, :],
+                    start=(g == 0),
+                    stop=(g == passes - 1),
+                )
+            result = results.tile([P, HD], F32, tag="result")
+            nc.scalar.copy(out=result[:], in_=acc[:])
+            nc.gpsimd.dma_start(out=out[b, h, tb * P : (tb + 1) * P, :], in_=result[:])
+
+        for i in range(len(heads) + 1):
+            if i < len(heads):
+                start_head(i)
+            for tb in range(TB):
+                if i < len(heads):
+                    mask_scores(i, tb)
+                if i > 0:
+                    finish_block(i - 1, tb)
+            if i < len(heads):
+                invert_row_sums(i)

@@ -10,7 +10,6 @@ U8 = mybir.dt.uint8
 FP8X4 = mybir.dt.float8_e4m3fn_x4
 MULT = mybir.AluOpType.mult
 MAX = mybir.AluOpType.max
-COPY = mybir.ActivationFunctionType.Copy
 
 B, NH, T, KD, HD = 4, 2, 1024, 128, 512
 P = 128
@@ -19,36 +18,43 @@ K_PASS = P * PACK
 TB = T // P
 BLOCKS_PER_CHUNK = K_PASS // P
 N_CHUNKS = T // K_PASS
+PSUM_BANKS = 8
+
+SCORES_AHEAD = 2
+TURN_BEHIND = 1
+REGROUP_BEHIND = 2
 
 FLOPS = 2 * B * NH * sum(K_PASS * K_PASS * (c + 1) for c in range(N_CHUNKS)) * (KD + HD)
+
+
+def passes_of(tb):
+    return tb // BLOCKS_PER_CHUNK + 1
 
 
 def tile_nucleusxmultiscaleretention_pb_t_kernel(tc, qr, kr, v, decay_mask, out):
     nc = tc.nc
     heads = [(b, h) for b in range(B) for h in range(NH)]
+    n_heads = len(heads)
 
     with ExitStack() as ctx:
-        const = ctx.enter_context(tc.tile_pool(name="const", bufs=1))
-        inputs = ctx.enter_context(tc.tile_pool(name="inputs", bufs=1))
+        fixed = ctx.enter_context(tc.tile_pool(name="fixed", bufs=1))
         per_head = ctx.enter_context(tc.tile_pool(name="per_head", bufs=2))
-        stream = ctx.enter_context(tc.tile_pool(name="stream", bufs=3))
         results = ctx.enter_context(tc.tile_pool(name="results", bufs=4))
-        psum_scores = ctx.enter_context(tc.psum_pool(name="psum_scores", bufs=3))
-        psum_turned = ctx.enter_context(tc.psum_pool(name="psum_turned", bufs=3))
-        psum_out = ctx.enter_context(tc.psum_pool(name="psum_out", bufs=2))
+        psum = ctx.enter_context(tc.psum_pool(name="psum", bufs=PSUM_BANKS))
+        ctx.enter_context(tc.manual_schedule())
 
-        q_rows, k_rows, v_rows, mask_tiles = [], [], [], {}
-        for i, (b, h) in enumerate(heads):
-            q_sb = inputs.tile([P, TB, KD], BF16, name="q_sb%d" % i)
+        q_rows, k_rows, v_rows, mask_tiles = {}, {}, {}, {}
+
+        def load_head(i):
+            b, h = heads[i]
+            q_sb = fixed.tile([P, TB, KD], BF16, name="q_sb%d" % i)
             nc.sync.dma_start(out=q_sb[:], in_=qr[b, h].rearrange("(n p) d -> p n d", p=P))
-            k_sb = inputs.tile([P, TB, KD], BF16, name="k_sb%d" % i)
+            k_sb = fixed.tile([P, TB, KD], BF16, name="k_sb%d" % i)
             nc.sync.dma_start(out=k_sb[:], in_=kr[b, h].rearrange("(n p) d -> p n d", p=P))
             if b == 0:
                 for c in range(N_CHUNKS):
                     keys = K_PASS * (c + 1)
-                    mask = inputs.tile(
-                        [P, BLOCKS_PER_CHUNK, keys], BF16, name="mask%d_%d" % (h, c)
-                    )
+                    mask = fixed.tile([P, BLOCKS_PER_CHUNK, keys], BF16, name="mask%d_%d" % (h, c))
                     nc.sync.dma_start(
                         out=mask[:],
                         in_=decay_mask[0, h, c * K_PASS : (c + 1) * K_PASS, 0:keys].rearrange(
@@ -56,161 +62,221 @@ def tile_nucleusxmultiscaleretention_pb_t_kernel(tc, qr, kr, v, decay_mask, out)
                         ),
                     )
                     mask_tiles[(h, c)] = mask
-            v_sb = inputs.tile([P, N_CHUNKS, PACK, HD], BF16, name="v_sb%d" % i)
+            v_sb = fixed.tile([P, N_CHUNKS, PACK, HD], BF16, name="v_sb%d" % i)
             nc.sync.dma_start(
                 out=v_sb[:].rearrange("p g (u e) n -> p (g u) (e n)", e=2),
                 in_=v[b, h].rearrange("(a p e) n -> p a (e n)", p=P, e=2),
             )
-            q_rows.append(q_sb)
-            k_rows.append(k_sb)
-            v_rows.append(v_sb)
+            q_rows[i], k_rows[i], v_rows[i] = q_sb, k_sb, v_sb
 
-        ident_bf = const.tile([P, P], BF16, name="ident_bf")
+        load_head(0)
+        load_head(1)
+
+        ident_bf = fixed.tile([P, P], BF16, name="ident_bf")
         make_identity(nc, ident_bf[:])
-        ident_f32 = const.tile([P, P], F32, name="ident_f32")
+        ident_f32 = fixed.tile([P, P], F32, name="ident_f32")
         make_identity(nc, ident_f32[:])
 
-        p_tiles = []
-        for half in range(2):
-            p_set = []
-            for tb in range(TB):
-                width = K_PASS * (tb // BLOCKS_PER_CHUNK + 1)
-                p_sb = const.tile([P, width], BF16, name="p_sb%d_%d" % (half, tb))
-                if (tb + 1) * P < width:
-                    nc.vector.memset(p_sb[:, (tb + 1) * P :], 0.0)
-                p_set.append(p_sb)
-            p_tiles.append(p_set)
+        p_sb, p_grouped, p_codes, p_scales = [], [], [], []
+        for tb in range(TB):
+            width = K_PASS * passes_of(tb)
+            p_tile = fixed.tile([P, width], BF16, name="p_sb%d" % tb)
+            if (tb + 1) * P < width:
+                nc.vector.memset(p_tile[:, (tb + 1) * P :], 0.0)
+            p_sb.append(p_tile)
+            p_grouped.append(
+                fixed.tile([P, width], BF16, name="p_grouped%d" % tb, align_bytes=64)
+            )
+            p_codes.append(
+                fixed.tile([P, width // PACK], U32, name="p_codes%d" % tb, align_bytes=64)
+            )
+            p_scales.append(
+                fixed.tile([P, width // PACK], U8, name="p_scales%d" % tb, align_bytes=64)
+            )
+        v_grouped = [
+            fixed.tile([P, HD * PACK], BF16, name="v_grouped%d" % g, align_bytes=64)
+            for g in range(N_CHUNKS)
+        ]
 
-        handed_on = {}
+        state = {}
 
-        def turn_rows(rows, tag):
-            turned_ps = psum_turned.tile([P, TB, P], BF16, tag="turned")
-            for n in range(TB):
-                nc.tensor.transpose(turned_ps[:, n, :], rows[:, n, :], ident_bf[:])
-            turned = per_head.tile([P, T], BF16, tag=tag, name=tag)
-            nc.scalar.copy(out=turned[:], in_=turned_ps[:].rearrange("d n t -> d (n t)"))
-            return turned
+        def turn_qk(i):
+            state[i] = {"scores": {}, "r": {}, "turned": {}, "acc": {}}
+            banks = []
+            for rows in (q_rows[i], k_rows[i]):
+                bank = psum.tile([P, TB, P], BF16, tag="bank", name="qk_bank")
+                for n in range(TB):
+                    nc.tensor.transpose(bank[:, n, :], rows[:, n, :], ident_bf[:])
+                banks.append(bank)
+            for key, bank in zip(("qT", "kT"), banks):
+                turned = per_head.tile([P, T], BF16, tag=key, name=key)
+                nc.scalar.copy(out=turned[:], in_=bank[:].rearrange("d n t -> d (n t)"))
+                state[i][key] = turned
+            state[i]["sums"] = per_head.tile([P, N_CHUNKS, TB], F32, tag="sums", name="sums")
 
-        def start_head(i):
-            state = {"qT": turn_rows(q_rows[i], "qT"), "kT": turn_rows(k_rows[i], "kT")}
-            v_codes = per_head.tile([P, N_CHUNKS, HD], U32, tag="v_codes", align_bytes=64)
-            v_scales = per_head.tile([P, N_CHUNKS, HD], U8, tag="v_scales", align_bytes=64)
-            grouped = []
-            for g in range(N_CHUNKS):
-                v_grouped = per_head.tile([P, HD * PACK], BF16, tag="v_grouped", align_bytes=64)
-                nc.vector.tensor_copy(
-                    out=v_grouped[:].rearrange("p (c i j) -> p c j i", i=4, j=PACK),
-                    in_=v_rows[i][:, g].rearrange("p j (c i) -> p c j i", i=4),
-                )
-                grouped.append(v_grouped)
-            for g in range(N_CHUNKS):
-                nc.vector.quantize_mx(
-                    out=v_codes[:, g, :].bitcast(FP8X4),
-                    scales=v_scales[:, g, :],
-                    in_=grouped[g][:],
-                )
-            state["v_codes"] = v_codes
-            state["v_scales"] = v_scales
-            state["sums"] = per_head.tile([P, N_CHUNKS, TB], F32, tag="sums", name="sums")
-            state["r"] = []
-            handed_on[i] = state
-
-        def mask_scores(i, tb):
-            state = handed_on[i]
-            h = heads[i][1]
-            mask = mask_tiles[(h, tb // BLOCKS_PER_CHUNK)]
-            keys = (tb + 1) * P
-            r_sb = per_head.tile([P, keys], F32, tag="r%d" % tb, name="r%d" % tb)
-            for g in range(tb // BLOCKS_PER_CHUNK + 1):
+        def scores(i, tb):
+            st = state[i]
+            banks = []
+            for g in range(passes_of(tb)):
                 lo = g * K_PASS
-                hi = min(keys, lo + K_PASS)
-                scores = psum_scores.tile([P, K_PASS], F32, tag="scores")
+                hi = min((tb + 1) * P, lo + K_PASS)
+                bank = psum.tile([P, K_PASS], F32, tag="bank", name="score_bank")
                 nc.tensor.matmul(
-                    scores[:, : hi - lo],
-                    lhsT=state["qT"][:, tb * P : (tb + 1) * P],
-                    rhs=state["kT"][:, lo:hi],
+                    bank[:, : hi - lo],
+                    lhsT=st["qT"][:, tb * P : (tb + 1) * P],
+                    rhs=st["kT"][:, lo:hi],
                     start=True,
                     stop=True,
                 )
+                banks.append(bank)
+            st["scores"][tb] = banks
+
+        def mask_scores(i, tb):
+            st = state[i]
+            mask = mask_tiles[(heads[i][1], tb // BLOCKS_PER_CHUNK)]
+            r_sb = per_head.tile([P, (tb + 1) * P], F32, tag="r%d" % tb, name="r%d" % tb)
+            for g, bank in enumerate(st["scores"][tb]):
+                lo = g * K_PASS
+                hi = min((tb + 1) * P, lo + K_PASS)
                 nc.vector.scalar_tensor_tensor(
                     out=r_sb[:, lo:hi],
-                    in0=scores[:, : hi - lo],
+                    in0=bank[:, : hi - lo],
                     scalar=1.0,
                     in1=mask[:, tb % BLOCKS_PER_CHUNK, lo:hi],
                     op0=MULT,
                     op1=MULT,
-                    accum_out=state["sums"][:, g, tb : tb + 1],
+                    accum_out=st["sums"][:, g, tb : tb + 1],
                 )
-            state["r"].append(r_sb)
+            st["r"][tb] = r_sb
 
         def invert_row_sums(i):
-            state = handed_on[i]
-            sums = state["sums"]
-            first = sums[:, 0, :]
+            st = state[i]
+            first = st["sums"][:, 0, :]
             late = slice(BLOCKS_PER_CHUNK, TB)
-            nc.vector.tensor_add(out=first[:, late], in0=first[:, late], in1=sums[:, 1, late])
-            clipped = per_head.tile([P, TB], F32, tag="clipped")
+            nc.vector.tensor_add(
+                out=first[:, late], in0=first[:, late], in1=st["sums"][:, 1, late]
+            )
+            clipped = per_head.tile([P, TB], F32, tag="clipped", name="clipped")
             nc.vector.tensor_scalar_max(out=clipped[:], in0=first, scalar1=1.0)
-            denom = per_head.tile([P, TB], F32, tag="denom")
+            denom = per_head.tile([P, TB], F32, tag="denom", name="denom")
             nc.vector.scalar_tensor_tensor(
                 out=denom[:], in0=first, scalar=-1.0, in1=clipped[:], op0=MULT, op1=MAX
             )
-            inverse = per_head.tile([P, TB], F32, tag="inverse")
+            inverse = per_head.tile([P, TB], F32, tag="inverse", name="inverse")
             nc.vector.reciprocal(out=inverse[:], in_=denom[:])
-            state["inverse"] = inverse
+            st["inverse"] = inverse
 
-        def finish_block(i, tb):
-            state = handed_on[i]
-            b, h = heads[i]
-            keys = (tb + 1) * P
-            passes = tb // BLOCKS_PER_CHUNK + 1
-            p_sb = p_tiles[i % 2][tb]
-            r_sb = state["r"][tb]
-            scale = state["inverse"][:, tb : tb + 1]
-            if tb % 3 == 0:
-                nc.vector.tensor_scalar_mul(out=p_sb[:, :keys], in0=r_sb[:], scalar1=scale)
-            else:
-                nc.scalar.activation(out=p_sb[:, :keys], in_=r_sb[:], func=COPY, scale=scale)
+        def scale_rows(i, tb):
+            st = state[i]
+            nc.gpsimd.tensor_scalar(
+                out=p_sb[tb][:, : (tb + 1) * P],
+                in0=st["r"][tb][:],
+                scalar1=st["inverse"][:, tb : tb + 1],
+                scalar2=1.0,
+                op0=MULT,
+                op1=MULT,
+            )
 
-            words = p_sb[:].bitcast(F32)
-            turned = psum_turned.tile([P, passes, 2, P], F32, tag="turned")
-            for g in range(passes):
+        def turn_p(i, tb):
+            words = p_sb[tb][:].bitcast(F32)
+            bank = psum.tile([P, passes_of(tb), 2, P], F32, tag="bank", name="p_bank")
+            for g in range(passes_of(tb)):
                 for u in range(2):
                     w0 = (2 * g + u) * P
-                    nc.tensor.transpose(turned[:, g, u, :], words[:, w0 : w0 + P], ident_f32[:])
-            p_grouped = stream.tile([P, passes * K_PASS], BF16, tag="p_grouped", align_bytes=64)
+                    nc.tensor.transpose(bank[:, g, u, :], words[:, w0 : w0 + P], ident_f32[:])
+            state[i]["turned"][tb] = bank
+
+        def regroup_p(i, tb):
             nc.scalar.copy(
-                out=p_grouped[:].bitcast(F32).rearrange("p (g t u) -> p g t u", g=passes, u=2),
-                in_=turned[:].rearrange("p g u t -> p g t u"),
-            )
-            p_codes = stream.tile([P, passes * P], U32, tag="p_codes", align_bytes=64)
-            p_scales = stream.tile([P, passes * P], U8, tag="p_scales", align_bytes=64)
-            nc.vector.quantize_mx(
-                out=p_codes[:].bitcast(FP8X4), scales=p_scales[:], in_=p_grouped[:]
+                out=p_grouped[tb][:]
+                .bitcast(F32)
+                .rearrange("p (g t u) -> p g t u", g=passes_of(tb), u=2),
+                in_=state[i]["turned"][tb][:].rearrange("p g u t -> p g t u"),
             )
 
-            acc = psum_out.tile([P, HD], F32, tag="acc")
-            for g in range(passes):
+        def quantise_p(tb):
+            nc.vector.quantize_mx(
+                out=p_codes[tb][:].bitcast(FP8X4), scales=p_scales[tb][:], in_=p_grouped[tb][:]
+            )
+
+        def regroup_v(i, g):
+            nc.vector.tensor_copy(
+                out=v_grouped[g][:].rearrange("p (c i j) -> p c j i", i=4, j=PACK),
+                in_=v_rows[i][:, g].rearrange("p j (c i) -> p c j i", i=4),
+            )
+
+        def quantise_v(i):
+            v_codes = per_head.tile([P, N_CHUNKS, HD], U32, tag="v_codes", align_bytes=64)
+            v_scales = per_head.tile([P, N_CHUNKS, HD], U8, tag="v_scales", align_bytes=64)
+            for g in range(N_CHUNKS):
+                nc.vector.quantize_mx(
+                    out=v_codes[:, g, :].bitcast(FP8X4),
+                    scales=v_scales[:, g, :],
+                    in_=v_grouped[g][:],
+                )
+            state[i]["v_codes"] = v_codes
+            state[i]["v_scales"] = v_scales
+
+        def multiply(i, tb):
+            st = state[i]
+            acc = psum.tile([P, HD], F32, tag="bank", name="acc")
+            for g in range(passes_of(tb)):
                 nc.tensor.matmul_mx(
                     out=acc[:],
-                    lhsT=p_codes[:, g * P : (g + 1) * P].bitcast(FP8X4),
-                    lhsT_scale=p_scales[:, g * P : (g + 1) * P],
-                    rhs=state["v_codes"][:, g, :].bitcast(FP8X4),
-                    rhs_scale=state["v_scales"][:, g, :],
+                    lhsT=p_codes[tb][:, g * P : (g + 1) * P].bitcast(FP8X4),
+                    lhsT_scale=p_scales[tb][:, g * P : (g + 1) * P],
+                    rhs=st["v_codes"][:, g, :].bitcast(FP8X4),
+                    rhs_scale=st["v_scales"][:, g, :],
                     start=(g == 0),
-                    stop=(g == passes - 1),
+                    stop=(g == passes_of(tb) - 1),
                 )
-            result = results.tile([P, HD], F32, tag="result")
-            nc.scalar.copy(out=result[:], in_=acc[:])
-            nc.gpsimd.dma_start(out=out[b, h, tb * P : (tb + 1) * P, :], in_=result[:])
+            st["acc"][tb] = acc
 
-        for i in range(len(heads) + 1):
-            if i < len(heads):
-                start_head(i)
-            for tb in range(TB):
-                if i < len(heads):
-                    mask_scores(i, tb)
-                if i > 0:
-                    finish_block(i - 1, tb)
-            if i < len(heads):
+        def store(i, tb):
+            b, h = heads[i]
+            result = results.tile([P, HD], F32, tag="result", name="result")
+            nc.scalar.copy(out=result[:], in_=state[i]["acc"][tb][:])
+            nc.sync.dma_start(out=out[b, h, tb * P : (tb + 1) * P, :], in_=result[:])
+
+        turn_qk(0)
+        for tb in range(SCORES_AHEAD):
+            scores(0, tb)
+
+        for i in range(n_heads + 1):
+            j = i - 1
+            masking = i < n_heads
+            finishing = j >= 0
+            if i + 2 < n_heads:
+                load_head(i + 2)
+
+            for step in range(TB + REGROUP_BEHIND):
+                if masking and step + SCORES_AHEAD < TB:
+                    scores(i, step + SCORES_AHEAD)
+                if finishing and step < TB:
+                    scale_rows(j, step)
+                if masking and step < TB:
+                    mask_scores(i, step)
+                if finishing and 0 <= step - TURN_BEHIND < TB:
+                    turn_p(j, step - TURN_BEHIND)
+                if finishing and 0 <= step - REGROUP_BEHIND < TB:
+                    regroup_p(j, step - REGROUP_BEHIND)
+
+            if i + 1 < n_heads:
+                turn_qk(i + 1)
+                for tb in range(SCORES_AHEAD):
+                    scores(i + 1, tb)
+            if masking:
+                for g in range(N_CHUNKS):
+                    regroup_v(i, g)
+            if finishing:
+                for tb in range(TB):
+                    quantise_p(tb)
+            if masking:
+                quantise_v(i)
                 invert_row_sums(i)
+            if finishing:
+                for tb in range(TB + 1):
+                    if tb < TB:
+                        multiply(j, tb)
+                    if tb > 0:
+                        store(j, tb - 1)

@@ -23,6 +23,9 @@ PSUM_BANKS = 8
 SCORES_AHEAD = 2
 TURN_BEHIND = 1
 REGROUP_BEHIND = 2
+TURN_QK_STEP = 5
+V_ON_SCALAR_STEP = 3
+V_PIECES = 2
 
 FLOPS = 2 * B * NH * sum(K_PASS * K_PASS * (c + 1) for c in range(N_CHUNKS)) * (KD + HD)
 
@@ -100,18 +103,22 @@ def tile_nucleusxmultiscaleretention_pb_t_kernel(tc, qr, kr, v, decay_mask, out)
 
         state = {}
 
-        def turn_qk(i):
+        def turn_rows(i, key):
+            rows = {"q": q_rows, "k": k_rows}[key][i]
+            bank = psum.tile([P, TB, P], BF16, tag="bank", name="qk_bank")
+            for n in range(TB):
+                nc.tensor.transpose(bank[:, n, :], rows[:, n, :], ident_bf[:])
+            state[i][key + "_bank"] = bank
+
+        def keep_turned(i, key):
+            turned = per_head.tile([P, T], BF16, tag=key + "T", name=key + "T")
+            nc.scalar.copy(
+                out=turned[:], in_=state[i][key + "_bank"][:].rearrange("d n t -> d (n t)")
+            )
+            state[i][key + "T"] = turned
+
+        def new_head(i):
             state[i] = {"scores": {}, "r": {}, "turned": {}, "acc": {}}
-            banks = []
-            for rows in (q_rows[i], k_rows[i]):
-                bank = psum.tile([P, TB, P], BF16, tag="bank", name="qk_bank")
-                for n in range(TB):
-                    nc.tensor.transpose(bank[:, n, :], rows[:, n, :], ident_bf[:])
-                banks.append(bank)
-            for key, bank in zip(("qT", "kT"), banks):
-                turned = per_head.tile([P, T], BF16, tag=key, name=key)
-                nc.scalar.copy(out=turned[:], in_=bank[:].rearrange("d n t -> d (n t)"))
-                state[i][key] = turned
             state[i]["sums"] = per_head.tile([P, N_CHUNKS, TB], F32, tag="sums", name="sums")
 
         def scores(i, tb):
@@ -166,16 +173,16 @@ def tile_nucleusxmultiscaleretention_pb_t_kernel(tc, qr, kr, v, decay_mask, out)
             nc.vector.reciprocal(out=inverse[:], in_=denom[:])
             st["inverse"] = inverse
 
-        def scale_rows(i, tb):
+        def scale_rows(i, tb, vector_is_free):
             st = state[i]
-            nc.gpsimd.tensor_scalar(
-                out=p_sb[tb][:, : (tb + 1) * P],
-                in0=st["r"][tb][:],
-                scalar1=st["inverse"][:, tb : tb + 1],
-                scalar2=1.0,
-                op0=MULT,
-                op1=MULT,
-            )
+            p_live = p_sb[tb][:, : (tb + 1) * P]
+            inverse = st["inverse"][:, tb : tb + 1]
+            if vector_is_free:
+                nc.vector.tensor_scalar_mul(out=p_live, in0=st["r"][tb][:], scalar1=inverse)
+            else:
+                nc.gpsimd.tensor_scalar(
+                    out=p_live, in0=st["r"][tb][:], scalar1=inverse, scalar2=1.0, op0=MULT, op1=MULT
+                )
 
         def turn_p(i, tb):
             words = p_sb[tb][:].bitcast(F32)
@@ -199,10 +206,12 @@ def tile_nucleusxmultiscaleretention_pb_t_kernel(tc, qr, kr, v, decay_mask, out)
                 out=p_codes[tb][:].bitcast(FP8X4), scales=p_scales[tb][:], in_=p_grouped[tb][:]
             )
 
-        def regroup_v(i, g):
-            nc.vector.tensor_copy(
-                out=v_grouped[g][:].rearrange("p (c i j) -> p c j i", i=4, j=PACK),
-                in_=v_rows[i][:, g].rearrange("p j (c i) -> p c j i", i=4),
+        def regroup_v(copy, i, g, n0, n1):
+            copy(
+                out=v_grouped[g][:, n0 * PACK : n1 * PACK].rearrange(
+                    "p (c i j) -> p c j i", i=4, j=PACK
+                ),
+                in_=v_rows[i][:, g, :, n0:n1].rearrange("p j (c i) -> p c j i", i=4),
             )
 
         def quantise_v(i):
@@ -238,7 +247,11 @@ def tile_nucleusxmultiscaleretention_pb_t_kernel(tc, qr, kr, v, decay_mask, out)
             nc.scalar.copy(out=result[:], in_=state[i]["acc"][tb][:])
             nc.sync.dma_start(out=out[b, h, tb * P : (tb + 1) * P, :], in_=result[:])
 
-        turn_qk(0)
+        new_head(0)
+        turn_rows(0, "q")
+        turn_rows(0, "k")
+        keep_turned(0, "q")
+        keep_turned(0, "k")
         for tb in range(SCORES_AHEAD):
             scores(0, tb)
 
@@ -252,22 +265,34 @@ def tile_nucleusxmultiscaleretention_pb_t_kernel(tc, qr, kr, v, decay_mask, out)
             for step in range(TB + REGROUP_BEHIND):
                 if masking and step + SCORES_AHEAD < TB:
                     scores(i, step + SCORES_AHEAD)
+                if i + 1 < n_heads:
+                    if step == TURN_QK_STEP:
+                        new_head(i + 1)
+                        turn_rows(i + 1, "q")
+                    if step == TURN_QK_STEP + 1:
+                        turn_rows(i + 1, "k")
+                        keep_turned(i + 1, "q")
+                    if step == TURN_QK_STEP + 2:
+                        keep_turned(i + 1, "k")
                 if finishing and step < TB:
-                    scale_rows(j, step)
+                    scale_rows(j, step, vector_is_free=not masking)
                 if masking and step < TB:
                     mask_scores(i, step)
                 if finishing and 0 <= step - TURN_BEHIND < TB:
                     turn_p(j, step - TURN_BEHIND)
                 if finishing and 0 <= step - REGROUP_BEHIND < TB:
                     regroup_p(j, step - REGROUP_BEHIND)
+                if masking and 0 <= step - V_ON_SCALAR_STEP < V_PIECES:
+                    piece = step - V_ON_SCALAR_STEP
+                    regroup_v(
+                        nc.scalar.copy, i, 1, piece * HD // V_PIECES, (piece + 1) * HD // V_PIECES
+                    )
 
             if i + 1 < n_heads:
-                turn_qk(i + 1)
                 for tb in range(SCORES_AHEAD):
                     scores(i + 1, tb)
             if masking:
-                for g in range(N_CHUNKS):
-                    regroup_v(i, g)
+                regroup_v(nc.vector.tensor_copy, i, 0, 0, HD)
             if finishing:
                 for tb in range(TB):
                     quantise_p(tb)

@@ -21,8 +21,8 @@ N_CHUNKS = T // K_PASS
 PSUM_BANKS = 8
 
 SCORES_AHEAD = 2
-TURN_BEHIND = 1
-REGROUP_BEHIND = 2
+TURN_BEHIND = 2
+REGROUP_BEHIND = 3
 TURN_QK_STEP = 5
 V_ON_SCALAR_STEP = 3
 V_PIECES = 2
@@ -156,22 +156,34 @@ def tile_nucleusxmultiscaleretention_pb_t_kernel(tc, qr, kr, v, decay_mask, out)
                 )
             st["r"][tb] = r_sb
 
-        def invert_row_sums(i):
-            st = state[i]
-            first = st["sums"][:, 0, :]
+        def join_row_sums(i):
+            first = state[i]["sums"][:, 0, :]
             late = slice(BLOCKS_PER_CHUNK, TB)
             nc.vector.tensor_add(
-                out=first[:, late], in0=first[:, late], in1=st["sums"][:, 1, late]
+                out=first[:, late], in0=first[:, late], in1=state[i]["sums"][:, 1, late]
             )
+
+        def clip_row_sums(i):
             clipped = per_head.tile([P, TB], F32, tag="clipped", name="clipped")
-            nc.vector.tensor_scalar_max(out=clipped[:], in0=first, scalar1=1.0)
+            nc.vector.tensor_scalar_max(out=clipped[:], in0=state[i]["sums"][:, 0, :], scalar1=1.0)
+            state[i]["clipped"] = clipped
+
+        def clip_negated_row_sums(i):
             denom = per_head.tile([P, TB], F32, tag="denom", name="denom")
             nc.vector.scalar_tensor_tensor(
-                out=denom[:], in0=first, scalar=-1.0, in1=clipped[:], op0=MULT, op1=MAX
+                out=denom[:],
+                in0=state[i]["sums"][:, 0, :],
+                scalar=-1.0,
+                in1=state[i]["clipped"][:],
+                op0=MULT,
+                op1=MAX,
             )
+            state[i]["denom"] = denom
+
+        def invert_row_sums(i):
             inverse = per_head.tile([P, TB], F32, tag="inverse", name="inverse")
-            nc.vector.reciprocal(out=inverse[:], in_=denom[:])
-            st["inverse"] = inverse
+            nc.vector.reciprocal(out=inverse[:], in_=state[i]["denom"][:])
+            state[i]["inverse"] = inverse
 
         def scale_rows(i, tb, vector_is_free):
             st = state[i]
@@ -292,11 +304,14 @@ def tile_nucleusxmultiscaleretention_pb_t_kernel(tc, qr, kr, v, decay_mask, out)
                 for tb in range(SCORES_AHEAD):
                     scores(i + 1, tb)
             if masking:
+                join_row_sums(i)
                 regroup_v(nc.vector.tensor_copy, i, 0, 0, HD)
+                clip_row_sums(i)
             if finishing:
                 for tb in range(TB):
                     quantise_p(tb)
             if masking:
+                clip_negated_row_sums(i)
                 quantise_v(i)
                 invert_row_sums(i)
             if finishing:

@@ -17,17 +17,19 @@ PACK = 4
 K_PASS = P * PACK
 TB = T // P
 BLOCKS_PER_CHUNK = K_PASS // P
-N_CHUNKS = T // K_PASS
+N_PASSES = T // K_PASS
 PSUM_BANKS = 8
 
 SCORES_AHEAD = 2
 TURN_BEHIND = 2
 REGROUP_BEHIND = 3
-TURN_QK_STEP = 5
-V_ON_SCALAR_STEP = 3
+TURN_QK_STEP = TB - 1 - SCORES_AHEAD
+V_ON_SCALAR_STEP = REGROUP_BEHIND
 V_PIECES = 2
+VECTOR_REGROUPS = TB - REGROUP_BEHIND
+QUANTISED_FIRST = 2
 
-FLOPS = 2 * B * NH * sum(K_PASS * K_PASS * (c + 1) for c in range(N_CHUNKS)) * (KD + HD)
+FLOPS = 2 * B * NH * sum(K_PASS * K_PASS * (c + 1) for c in range(N_PASSES)) * (KD + HD)
 
 
 def passes_of(tb):
@@ -55,7 +57,7 @@ def tile_nucleusxmultiscaleretention_pb_t_kernel(tc, qr, kr, v, decay_mask, out)
             k_sb = fixed.tile([P, TB, KD], BF16, name="k_sb%d" % i)
             nc.sync.dma_start(out=k_sb[:], in_=kr[b, h].rearrange("(n p) d -> p n d", p=P))
             if b == 0:
-                for c in range(N_CHUNKS):
+                for c in range(N_PASSES):
                     keys = K_PASS * (c + 1)
                     mask = fixed.tile([P, BLOCKS_PER_CHUNK, keys], BF16, name="mask%d_%d" % (h, c))
                     nc.sync.dma_start(
@@ -65,7 +67,7 @@ def tile_nucleusxmultiscaleretention_pb_t_kernel(tc, qr, kr, v, decay_mask, out)
                         ),
                     )
                     mask_tiles[(h, c)] = mask
-            v_sb = fixed.tile([P, N_CHUNKS, PACK, HD], BF16, name="v_sb%d" % i)
+            v_sb = fixed.tile([P, N_PASSES, PACK, HD], BF16, name="v_sb%d" % i)
             nc.sync.dma_start(
                 out=v_sb[:].rearrange("p g (u e) n -> p (g u) (e n)", e=2),
                 in_=v[b, h].rearrange("(a p e) n -> p a (e n)", p=P, e=2),
@@ -98,10 +100,14 @@ def tile_nucleusxmultiscaleretention_pb_t_kernel(tc, qr, kr, v, decay_mask, out)
             )
         v_grouped = [
             fixed.tile([P, HD * PACK], BF16, name="v_grouped%d" % g, align_bytes=64)
-            for g in range(N_CHUNKS)
+            for g in range(N_PASSES)
         ]
 
         state = {}
+
+        def new_head(i):
+            state[i] = {"scores": {}, "r": {}, "p_bank": {}, "acc": {}}
+            state[i]["sums"] = per_head.tile([P, N_PASSES, TB], F32, tag="sums", name="sums")
 
         def turn_rows(i, key):
             rows = {"q": q_rows, "k": k_rows}[key][i]
@@ -116,10 +122,6 @@ def tile_nucleusxmultiscaleretention_pb_t_kernel(tc, qr, kr, v, decay_mask, out)
                 out=turned[:], in_=state[i][key + "_bank"][:].rearrange("d n t -> d (n t)")
             )
             state[i][key + "T"] = turned
-
-        def new_head(i):
-            state[i] = {"scores": {}, "r": {}, "turned": {}, "acc": {}}
-            state[i]["sums"] = per_head.tile([P, N_CHUNKS, TB], F32, tag="sums", name="sums")
 
         def scores(i, tb):
             st = state[i]
@@ -198,19 +200,20 @@ def tile_nucleusxmultiscaleretention_pb_t_kernel(tc, qr, kr, v, decay_mask, out)
 
         def turn_p(i, tb):
             words = p_sb[tb][:].bitcast(F32)
-            bank = psum.tile([P, passes_of(tb), 2, P], F32, tag="bank", name="p_bank")
+            p_bank = psum.tile([P, passes_of(tb), 2, P], F32, tag="bank", name="p_bank")
             for g in range(passes_of(tb)):
                 for u in range(2):
                     w0 = (2 * g + u) * P
-                    nc.tensor.transpose(bank[:, g, u, :], words[:, w0 : w0 + P], ident_f32[:])
-            state[i]["turned"][tb] = bank
+                    nc.tensor.transpose(p_bank[:, g, u, :], words[:, w0 : w0 + P], ident_f32[:])
+            state[i]["p_bank"][tb] = p_bank
 
         def regroup_p(i, tb):
-            nc.scalar.copy(
+            copy = nc.vector.tensor_copy if tb == VECTOR_REGROUPS else nc.scalar.copy
+            copy(
                 out=p_grouped[tb][:]
                 .bitcast(F32)
                 .rearrange("p (g t u) -> p g t u", g=passes_of(tb), u=2),
-                in_=state[i]["turned"][tb][:].rearrange("p g u t -> p g t u"),
+                in_=state[i]["p_bank"][tb][:].rearrange("p g u t -> p g t u"),
             )
 
         def quantise_p(tb):
@@ -226,17 +229,19 @@ def tile_nucleusxmultiscaleretention_pb_t_kernel(tc, qr, kr, v, decay_mask, out)
                 in_=v_rows[i][:, g, :, n0:n1].rearrange("p j (c i) -> p c j i", i=4),
             )
 
-        def quantise_v(i):
-            v_codes = per_head.tile([P, N_CHUNKS, HD], U32, tag="v_codes", align_bytes=64)
-            v_scales = per_head.tile([P, N_CHUNKS, HD], U8, tag="v_scales", align_bytes=64)
-            for g in range(N_CHUNKS):
-                nc.vector.quantize_mx(
-                    out=v_codes[:, g, :].bitcast(FP8X4),
-                    scales=v_scales[:, g, :],
-                    in_=v_grouped[g][:],
+        def quantise_v(i, g):
+            if g == 0:
+                state[i]["v_codes"] = per_head.tile(
+                    [P, N_PASSES, HD], U32, tag="v_codes", name="v_codes", align_bytes=64
                 )
-            state[i]["v_codes"] = v_codes
-            state[i]["v_scales"] = v_scales
+                state[i]["v_scales"] = per_head.tile(
+                    [P, N_PASSES, HD], U8, tag="v_scales", name="v_scales", align_bytes=64
+                )
+            nc.vector.quantize_mx(
+                out=state[i]["v_codes"][:, g, :].bitcast(FP8X4),
+                scales=state[i]["v_scales"][:, g, :],
+                in_=v_grouped[g][:],
+            )
 
         def multiply(i, tb):
             st = state[i]
@@ -305,15 +310,20 @@ def tile_nucleusxmultiscaleretention_pb_t_kernel(tc, qr, kr, v, decay_mask, out)
                     scores(i + 1, tb)
             if masking:
                 join_row_sums(i)
-                regroup_v(nc.vector.tensor_copy, i, 0, 0, HD)
-                clip_row_sums(i)
             if finishing:
-                for tb in range(TB):
+                for tb in range(QUANTISED_FIRST):
+                    quantise_p(tb)
+            if masking:
+                clip_row_sums(i)
+                regroup_v(nc.vector.tensor_copy, i, 0, 0, HD)
+            if finishing:
+                for tb in range(QUANTISED_FIRST, TB):
                     quantise_p(tb)
             if masking:
                 clip_negated_row_sums(i)
-                quantise_v(i)
+                quantise_v(i, 0)
                 invert_row_sums(i)
+                quantise_v(i, 1)
             if finishing:
                 for tb in range(TB + 1):
                     if tb < TB:

@@ -44,7 +44,7 @@ def tile_nucleusxmultiscaleretention_pb_t_kernel(tc, qr, kr, v, decay_mask, out)
     with ExitStack() as ctx:
         fixed = ctx.enter_context(tc.tile_pool(name="fixed", bufs=1))
         per_head = ctx.enter_context(tc.tile_pool(name="per_head", bufs=2))
-        results = ctx.enter_context(tc.tile_pool(name="results", bufs=4))
+        results = ctx.enter_context(tc.tile_pool(name="results", bufs=TB))
         psum = ctx.enter_context(tc.psum_pool(name="psum", bufs=PSUM_BANKS))
         ctx.enter_context(tc.manual_schedule())
 

@@ -103,11 +103,20 @@ def tile_nucleusxmultiscaleretention_pb_t_kernel(tc, qr, kr, v, decay_mask, out)
             for g in range(N_PASSES)
         ]
 
+        row_sums = []
+        for n in range(2):
+            sums = fixed.tile([P, TB, 2], F32, name="row_sums%d" % n)
+            nc.vector.memset(sums[:], 1.0)
+            row_sums.append(sums)
+
         state = {}
 
         def new_head(i):
             state[i] = {"scores": {}, "r": {}, "p_bank": {}, "acc": {}}
-            state[i]["sums"] = per_head.tile([P, N_PASSES, TB], F32, tag="sums", name="sums")
+            state[i]["sums"] = row_sums[i % 2]
+            state[i]["second_sums"] = per_head.tile(
+                [P, TB - BLOCKS_PER_CHUNK], F32, tag="second_sums", name="second_sums"
+            )
 
         def turn_rows(i, key):
             rows = {"q": q_rows, "k": k_rows}[key][i]
@@ -154,31 +163,26 @@ def tile_nucleusxmultiscaleretention_pb_t_kernel(tc, qr, kr, v, decay_mask, out)
                     in1=mask[:, tb % BLOCKS_PER_CHUNK, lo:hi],
                     op0=MULT,
                     op1=MULT,
-                    accum_out=st["sums"][:, g, tb : tb + 1],
+                    accum_out=(
+                        st["sums"][:, tb, 0:1]
+                        if g == 0
+                        else st["second_sums"][:, tb - BLOCKS_PER_CHUNK : tb - BLOCKS_PER_CHUNK + 1]
+                    ),
                 )
             st["r"][tb] = r_sb
 
         def join_row_sums(i):
-            first = state[i]["sums"][:, 0, :]
-            late = slice(BLOCKS_PER_CHUNK, TB)
-            nc.vector.tensor_add(
-                out=first[:, late], in0=first[:, late], in1=state[i]["sums"][:, 1, late]
-            )
+            first = state[i]["sums"][:, BLOCKS_PER_CHUNK:, 0]
+            nc.vector.tensor_add(out=first, in0=first, in1=state[i]["second_sums"][:])
 
         def clip_row_sums(i):
-            clipped = per_head.tile([P, TB], F32, tag="clipped", name="clipped")
-            nc.vector.tensor_scalar_max(out=clipped[:], in0=state[i]["sums"][:, 0, :], scalar1=1.0)
-            state[i]["clipped"] = clipped
-
-        def clip_negated_row_sums(i):
             denom = per_head.tile([P, TB], F32, tag="denom", name="denom")
-            nc.vector.scalar_tensor_tensor(
+            nc.vector.tensor_reduce(
                 out=denom[:],
-                in0=state[i]["sums"][:, 0, :],
-                scalar=-1.0,
-                in1=state[i]["clipped"][:],
-                op0=MULT,
-                op1=MAX,
+                in_=state[i]["sums"][:],
+                op=MAX,
+                axis=mybir.AxisListType.X,
+                apply_absolute_value=True,
             )
             state[i]["denom"] = denom
 
@@ -208,7 +212,7 @@ def tile_nucleusxmultiscaleretention_pb_t_kernel(tc, qr, kr, v, decay_mask, out)
             state[i]["p_bank"][tb] = p_bank
 
         def regroup_p(i, tb):
-            copy = nc.vector.tensor_copy if tb == VECTOR_REGROUPS else nc.scalar.copy
+            copy = nc.scalar.copy
             copy(
                 out=p_grouped[tb][:]
                 .bitcast(F32)
@@ -314,13 +318,12 @@ def tile_nucleusxmultiscaleretention_pb_t_kernel(tc, qr, kr, v, decay_mask, out)
                 for tb in range(QUANTISED_FIRST):
                     quantise_p(tb)
             if masking:
-                clip_row_sums(i)
                 regroup_v(nc.vector.tensor_copy, i, 0, 0, HD)
             if finishing:
                 for tb in range(QUANTISED_FIRST, TB):
                     quantise_p(tb)
             if masking:
-                clip_negated_row_sums(i)
+                clip_row_sums(i)
                 quantise_v(i, 0)
                 invert_row_sums(i)
                 quantise_v(i, 1)

@@ -20,6 +20,32 @@ BLOCKS_PER_CHUNK = K_PASS // P
 N_PASSES = T // K_PASS
 PSUM_BANKS = 8
 
+EARLY = (6, 7)
+PREFETCH = 3
+FIRST_EARLY = 2
+TM0 = 7
+V_VECTOR = 0
+def V_REGROUPS(i):
+    return ()
+def G_WORK(i):
+    if i <= 2:
+        return {}
+    return {6: [(i, 1, 0, 512)]}
+def S_WORK(i):
+    if i == 0:
+        return {7: [(0, 1, 0, 512)]}
+    if i == 1:
+        return {0: [(0, 0, 0, 256)], 3: [(0, 0, 256, 512)], 10: [(1, 1, 256, 512)]}
+    if i == 2:
+        return {3: [(2, 1, 128, 512)]}
+    return {3: [(i, 1, 512, 512)] if 512 < 512 else [], 4: [(i, 0, 320, 512)] if 192 else []}
+def V_WORK(i):
+    if i == 1:
+        return [(i, 0, 0, 512), (i, 1, 0, 256)]
+    if i == 2:
+        return [(i, 0, 0, 512), (i, 1, 0, 128)]
+    return [(i, 0, 0, 320)]
+
 SCORES_AHEAD = 2
 TURN_BEHIND = 2
 REGROUP_BEHIND = 3
@@ -38,98 +64,149 @@ def passes_of(tb):
 
 def tile_nucleusxmultiscaleretention_pb_t_kernel(tc, qr, kr, v, decay_mask, out):
     nc = tc.nc
-    heads = [(b, h) for b in range(B) for h in range(NH)]
+    heads = [(b, h) for h in range(NH) for b in range(B)]
     n_heads = len(heads)
 
     with ExitStack() as ctx:
         fixed = ctx.enter_context(tc.tile_pool(name="fixed", bufs=1))
         per_head = ctx.enter_context(tc.tile_pool(name="per_head", bufs=2))
         results = ctx.enter_context(tc.tile_pool(name="results", bufs=TB))
+        r_pool = ctx.enter_context(tc.tile_pool(name="r_pool", bufs=2))
+        rows_pool = ctx.enter_context(tc.tile_pool(name="rows_pool", bufs=4))
+        r_once = ctx.enter_context(tc.tile_pool(name="r_once", bufs=1))
+        mt_pool = ctx.enter_context(tc.tile_pool(name="mt_pool", bufs=1))
         psum = ctx.enter_context(tc.psum_pool(name="psum", bufs=PSUM_BANKS))
         ctx.enter_context(tc.manual_schedule())
 
         q_rows, k_rows, v_rows, mask_tiles = {}, {}, {}, {}
 
-        def load_head(i):
+        def load_rows(i, c):
             b, h = heads[i]
-            q_sb = fixed.tile([P, TB, KD], BF16, name="q_sb%d" % i)
-            nc.sync.dma_start(out=q_sb[:], in_=qr[b, h].rearrange("(n p) d -> p n d", p=P))
-            k_sb = fixed.tile([P, TB, KD], BF16, name="k_sb%d" % i)
-            nc.sync.dma_start(out=k_sb[:], in_=kr[b, h].rearrange("(n p) d -> p n d", p=P))
-            if b == 0:
-                for c in range(N_PASSES):
-                    keys = K_PASS * (c + 1)
-                    mask = fixed.tile([P, BLOCKS_PER_CHUNK, keys], BF16, name="mask%d_%d" % (h, c))
-                    nc.sync.dma_start(
-                        out=mask[:],
-                        in_=decay_mask[0, h, c * K_PASS : (c + 1) * K_PASS, 0:keys].rearrange(
-                            "(n p) s -> p n s", p=P
-                        ),
-                    )
-                    mask_tiles[(h, c)] = mask
-            v_sb = fixed.tile([P, N_PASSES, PACK, HD], BF16, name="v_sb%d" % i)
-            nc.sync.dma_start(
-                out=v_sb[:].rearrange("p g (u e) n -> p (g u) (e n)", e=2),
-                in_=v[b, h].rearrange("(a p e) n -> p a (e n)", p=P, e=2),
-            )
-            q_rows[i], k_rows[i], v_rows[i] = q_sb, k_sb, v_sb
+            for key, kept, dram in (("q", q_rows, qr), ("k", k_rows, kr)):
+                sb = rows_pool.tile([P, BLOCKS_PER_CHUNK, KD], BF16, tag=key + "_rows%d" % c, name=key + "_rows")
+                nc.sync.dma_start(
+                    out=sb[:],
+                    in_=dram[b, h, c * K_PASS : (c + 1) * K_PASS].rearrange("(n p) d -> p n d", p=P),
+                )
+                kept[(i, c)] = sb
 
-        load_head(0)
-        load_head(1)
+        def load_mask(h, pair):
+            keys = 2 * (pair + 1) * P
+            mask = fixed.tile([P, 2, keys], BF16, name="mask%d_%d" % (h, pair))
+            nc.sync.dma_start(
+                out=mask[:],
+                in_=decay_mask[0, h, 2 * pair * P : 2 * (pair + 1) * P, 0:keys].rearrange(
+                    "(n p) s -> p n s", p=P
+                ),
+            )
+            mask_tiles[(h, pair)] = mask
+
+        def load_v(i, g):
+            b, h = heads[i]
+            v_sb = rows_pool.tile([P, PACK, HD], BF16, tag="v_rows%d" % g, name="v_rows")
+            nc.sync.dma_start(
+                out=v_sb[:].rearrange("p (u e) n -> p u (e n)", e=2),
+                in_=v[b, h, g * K_PASS : (g + 1) * K_PASS].rearrange("(a p e) n -> p a (e n)", p=P, e=2),
+            )
+            v_rows[(i, g)] = v_sb
+
+        load_rows(0, 0)
+        load_mask(0, 0)
+        load_rows(0, 1)
+        load_mask(0, 1)
+        load_mask(0, 2)
+        load_mask(0, 3)
+        load_rows(1, 0)
+        load_rows(1, 1)
+        load_v(0, 1)
+        load_v(0, 0)
+        load_rows(2, 0)
+        load_rows(2, 1)
+        load_v(1, 1)
+        load_v(1, 0)
 
         ident_bf = fixed.tile([P, P], BF16, name="ident_bf")
         make_identity(nc, ident_bf[:])
         ident_f32 = fixed.tile([P, P], F32, name="ident_f32")
         make_identity(nc, ident_f32[:])
 
-        p_sb, p_grouped, p_codes, p_scales = [], [], [], []
+        p_sb, p_codes, p_scales, p_grouped = [], [], [], {}
         for tb in range(TB):
             width = K_PASS * passes_of(tb)
-            p_tile = fixed.tile([P, width], BF16, name="p_sb%d" % tb)
-            if (tb + 1) * P < width:
-                nc.vector.memset(p_tile[:, (tb + 1) * P :], 0.0)
-            p_sb.append(p_tile)
-            p_grouped.append(
-                fixed.tile([P, width], BF16, name="p_grouped%d" % tb, align_bytes=64)
-            )
+            p_sb.append([])
+            for n in range(2 if tb in EARLY else 1):
+                p_tile = fixed.tile([P, width], BF16, name="p_sb%d_%d" % (tb, n))
+                if (tb + 1) * P < width:
+                    nc.vector.memset(p_tile[:, (tb + 1) * P :], 0.0)
+                p_sb[tb].append(p_tile)
             p_codes.append(
                 fixed.tile([P, width // PACK], U32, name="p_codes%d" % tb, align_bytes=64)
             )
             p_scales.append(
                 fixed.tile([P, width // PACK], U8, name="p_scales%d" % tb, align_bytes=64)
             )
-        v_grouped = [
-            fixed.tile([P, HD * PACK], BF16, name="v_grouped%d" % g, align_bytes=64)
-            for g in range(N_PASSES)
-        ]
+        v_grouped = {}
+        row_sums = fixed.tile([P, TB + len(EARLY), 2], F32, name="row_sums")
+        nc.vector.memset(row_sums[:], 1.0)
+        unread = fixed.tile([P, KD], F32, name="unread")
+        mask_turned = {}
 
-        row_sums = []
-        for n in range(2):
-            sums = fixed.tile([P, TB, 2], F32, name="row_sums%d" % n)
-            nc.vector.memset(sums[:], 1.0)
-            row_sums.append(sums)
+        def early(i):
+            return EARLY if i >= FIRST_EARLY else ()
+
+        def turn_mask(h, e):
+            if e == 0:
+                mask_turned[h] = mt_pool.tile([P, len(EARLY), TB, P], BF16, tag="mask_turned%d" % h, name="mask_turned")
+            turned = mask_turned[h]
+            tb = EARLY[e]
+            bank = psum.tile([P, TB, P], BF16, tag="bank", name="mask_bank")
+            for sb in range(tb + 1):
+                nc.tensor.transpose(
+                    bank[:, sb, :], mask_tiles[(h, tb // 2)][:, tb % 2, sb * P : (sb + 1) * P], ident_bf[:]
+                )
+            nc.scalar.copy(out=turned[:, e, : tb + 1, :].rearrange("s n t -> s (n t)"), in_=bank[:, : tb + 1, :].rearrange("s n t -> s (n t)"))
+
+        def early_sums(i):
+            bank = psum.tile([P, len(EARLY), KD], F32, tag="bank", name="mk_bank")
+            turned = mask_turned[heads[i][1]]
+            for e, tb in enumerate(EARLY):
+                for sb in range(tb + 1):
+                    nc.tensor.matmul(
+                        bank[:, e, :],
+                        lhsT=turned[:, e, sb, :],
+                        rhs=k_rows[(i, sb // BLOCKS_PER_CHUNK)][:, sb % BLOCKS_PER_CHUNK, :],
+                        start=(sb == 0),
+                        stop=(sb == tb),
+                    )
+            state[i]["mk_bank"] = bank
+
+        def early_sums2(i):
+            for e, tb in enumerate(EARLY):
+                nc.vector.scalar_tensor_tensor(
+                    out=unread[:],
+                    in0=state[i]["mk_bank"][:, e, :],
+                    scalar=1.0,
+                    in1=q_rows[(i, tb // BLOCKS_PER_CHUNK)][:, tb % BLOCKS_PER_CHUNK, :],
+                    op0=MULT,
+                    op1=MULT,
+                    accum_out=row_sums[:, TB + e, 0:1],
+                )
 
         state = {}
+        gps = lambda out, in_: nc.gpsimd.tensor_scalar(out=out, in0=in_, scalar1=1.0, scalar2=0.0, op0=MULT, op1=mybir.AluOpType.add)
+        for i in range(n_heads):
+            state[i] = {"scores": {}, "r": {}, "p_bank": {}, "acc": {}, "inverse": {}, "second_sums": {}}
 
-        def new_head(i):
-            state[i] = {"scores": {}, "r": {}, "p_bank": {}, "acc": {}}
-            state[i]["sums"] = row_sums[i % 2]
-            state[i]["second_sums"] = per_head.tile(
-                [P, TB - BLOCKS_PER_CHUNK], F32, tag="second_sums", name="second_sums"
-            )
-
-        def turn_rows(i, key):
-            rows = {"q": q_rows, "k": k_rows}[key][i]
+        def turn_all(i, key):
+            rows = {"q": q_rows, "k": k_rows}[key]
             bank = psum.tile([P, TB, P], BF16, tag="bank", name="qk_bank")
             for n in range(TB):
-                nc.tensor.transpose(bank[:, n, :], rows[:, n, :], ident_bf[:])
+                nc.tensor.transpose(bank[:, n, :], rows[(i, n // BLOCKS_PER_CHUNK)][:, n % BLOCKS_PER_CHUNK, :], ident_bf[:])
             state[i][key + "_bank"] = bank
 
-        def keep_turned(i, key):
+        def keep_turned(copy, i, key):
             turned = per_head.tile([P, T], BF16, tag=key + "T", name=key + "T")
-            nc.scalar.copy(
-                out=turned[:], in_=state[i][key + "_bank"][:].rearrange("d n t -> d (n t)")
-            )
+            copy(out=turned[:], in_=state[i][key + "_bank"][:].rearrange("d n t -> d (n t)"))
             state[i][key + "T"] = turned
 
         def scores(i, tb):
@@ -151,59 +228,80 @@ def tile_nucleusxmultiscaleretention_pb_t_kernel(tc, qr, kr, v, decay_mask, out)
 
         def mask_scores(i, tb):
             st = state[i]
-            mask = mask_tiles[(heads[i][1], tb // BLOCKS_PER_CHUNK)]
-            r_sb = per_head.tile([P, (tb + 1) * P], F32, tag="r%d" % tb, name="r%d" % tb)
+            mask = mask_tiles[(heads[i][1], tb // 2)]
+            is_early = tb in early(i)
+            if not is_early:
+                r_sb = (r_once if tb in EARLY else r_pool).tile([P, (tb + 1) * P], F32, tag="r%d" % tb, name="r%d" % tb)
+                st["r"][tb] = r_sb
             for g, bank in enumerate(st["scores"][tb]):
                 lo = g * K_PASS
                 hi = min((tb + 1) * P, lo + K_PASS)
-                nc.vector.scalar_tensor_tensor(
-                    out=r_sb[:, lo:hi],
-                    in0=bank[:, : hi - lo],
-                    scalar=1.0,
-                    in1=mask[:, tb % BLOCKS_PER_CHUNK, lo:hi],
-                    op0=MULT,
-                    op1=MULT,
-                    accum_out=(
-                        st["sums"][:, tb, 0:1]
-                        if g == 0
-                        else st["second_sums"][:, tb - BLOCKS_PER_CHUNK : tb - BLOCKS_PER_CHUNK + 1]
-                    ),
-                )
-            st["r"][tb] = r_sb
+                if is_early:
+                    nc.vector.scalar_tensor_tensor(
+                        out=p_of(i, tb)[:, lo:hi],
+                        in0=bank[:, : hi - lo],
+                        scalar=st["inverse"][tb],
+                        in1=mask[:, tb % 2, lo:hi],
+                        op0=MULT,
+                        op1=MULT,
+                    )
+                else:
+                    if g == 0:
+                        row_sum = row_sums[:, tb, 0:1]
+                    else:
+                        row_sum = second_sums[:, tb - BLOCKS_PER_CHUNK : tb - BLOCKS_PER_CHUNK + 1]
+                    nc.vector.scalar_tensor_tensor(
+                        out=r_sb[:, lo:hi],
+                        in0=bank[:, : hi - lo],
+                        scalar=1.0,
+                        in1=mask[:, tb % 2, lo:hi],
+                        op0=MULT,
+                        op1=MULT,
+                        accum_out=row_sum,
+                    )
+
+        second_sums = fixed.tile([P, BLOCKS_PER_CHUNK], F32, name="second_sums")
 
         def join_row_sums(i):
-            first = state[i]["sums"][:, BLOCKS_PER_CHUNK:, 0]
-            nc.vector.tensor_add(out=first, in0=first, in1=state[i]["second_sums"][:])
+            n = TB - BLOCKS_PER_CHUNK - len(early(i))
+            first = row_sums[:, BLOCKS_PER_CHUNK : BLOCKS_PER_CHUNK + n, 0]
+            nc.vector.tensor_add(out=first, in0=first, in1=second_sums[:, :n])
 
-        def clip_row_sums(i):
-            denom = per_head.tile([P, TB], F32, tag="denom", name="denom")
+        denom = {}
+
+        def clip_row_sums():
+            denom[0] = per_head.tile([P, TB + len(EARLY)], F32, tag="denom", name="denom")
             nc.vector.tensor_reduce(
-                out=denom[:],
-                in_=state[i]["sums"][:],
+                out=denom[0][:],
+                in_=row_sums[:],
                 op=MAX,
                 axis=mybir.AxisListType.X,
                 apply_absolute_value=True,
             )
-            state[i]["denom"] = denom
 
         def invert_row_sums(i):
-            inverse = per_head.tile([P, TB], F32, tag="inverse", name="inverse")
-            nc.vector.reciprocal(out=inverse[:], in_=state[i]["denom"][:])
-            state[i]["inverse"] = inverse
+            inverse = per_head.tile([P, TB + len(EARLY)], F32, tag="inverse", name="inverse")
+            nc.vector.reciprocal(out=inverse[:], in_=denom[0][:])
+            for tb in range(TB):
+                if tb not in early(i):
+                    state[i]["inverse"][tb] = inverse[:, tb : tb + 1]
+            if i + 1 < n_heads and early(i + 1):
+                for e, tb in enumerate(EARLY):
+                    state[i + 1]["inverse"][tb] = inverse[:, TB + e : TB + e + 1]
 
-        def scale_rows(i, tb, vector_is_free):
+        def p_of(i, tb):
+            return p_sb[tb][i % len(p_sb[tb])]
+
+        def scale_rows(engine, i, tb):
             st = state[i]
-            p_live = p_sb[tb][:, : (tb + 1) * P]
-            inverse = st["inverse"][:, tb : tb + 1]
-            if vector_is_free:
-                nc.vector.tensor_scalar_mul(out=p_live, in0=st["r"][tb][:], scalar1=inverse)
-            else:
-                nc.gpsimd.tensor_scalar(
-                    out=p_live, in0=st["r"][tb][:], scalar1=inverse, scalar2=1.0, op0=MULT, op1=MULT
-                )
+            p_live = p_of(i, tb)[:, : (tb + 1) * P]
+            inverse = st["inverse"][tb]
+            engine.tensor_scalar(
+                out=p_live, in0=st["r"][tb][:], scalar1=inverse, scalar2=1.0, op0=MULT, op1=MULT
+            )
 
         def turn_p(i, tb):
-            words = p_sb[tb][:].bitcast(F32)
+            words = p_of(i, tb)[:].bitcast(F32)
             p_bank = psum.tile([P, passes_of(tb), 2, P], F32, tag="bank", name="p_bank")
             for g in range(passes_of(tb)):
                 for u in range(2):
@@ -211,8 +309,9 @@ def tile_nucleusxmultiscaleretention_pb_t_kernel(tc, qr, kr, v, decay_mask, out)
                     nc.tensor.transpose(p_bank[:, g, u, :], words[:, w0 : w0 + P], ident_f32[:])
             state[i]["p_bank"][tb] = p_bank
 
-        def regroup_p(i, tb):
-            copy = nc.scalar.copy
+        def regroup_p(copy, i, tb):
+            p_grouped[tb] = per_head.tile([P, K_PASS * passes_of(tb)], BF16, tag="p_grouped%d" % tb, name="p_grouped", align_bytes=64)
+            p_kept[(i, tb)] = p_grouped[tb]
             copy(
                 out=p_grouped[tb][:]
                 .bitcast(F32)
@@ -220,17 +319,21 @@ def tile_nucleusxmultiscaleretention_pb_t_kernel(tc, qr, kr, v, decay_mask, out)
                 in_=state[i]["p_bank"][tb][:].rearrange("p g u t -> p g t u"),
             )
 
-        def quantise_p(tb):
+        p_kept = {}
+
+        def quantise_p(i, tb):
             nc.vector.quantize_mx(
-                out=p_codes[tb][:].bitcast(FP8X4), scales=p_scales[tb][:], in_=p_grouped[tb][:]
+                out=p_codes[tb][:].bitcast(FP8X4), scales=p_scales[tb][:], in_=p_kept[(i, tb)][:]
             )
 
         def regroup_v(copy, i, g, n0, n1):
+            if (i, g) not in v_grouped:
+                v_grouped[(i, g)] = per_head.tile([P, HD * PACK], BF16, tag="v_grouped%d" % g, name="v_grouped", align_bytes=64)
             copy(
-                out=v_grouped[g][:, n0 * PACK : n1 * PACK].rearrange(
+                out=v_grouped[(i, g)][:, n0 * PACK : n1 * PACK].rearrange(
                     "p (c i j) -> p c j i", i=4, j=PACK
                 ),
-                in_=v_rows[i][:, g, :, n0:n1].rearrange("p j (c i) -> p c j i", i=4),
+                in_=v_rows[(i, g)][:, :, n0:n1].rearrange("p j (c i) -> p c j i", i=4),
             )
 
         def quantise_v(i, g):
@@ -244,7 +347,7 @@ def tile_nucleusxmultiscaleretention_pb_t_kernel(tc, qr, kr, v, decay_mask, out)
             nc.vector.quantize_mx(
                 out=state[i]["v_codes"][:, g, :].bitcast(FP8X4),
                 scales=state[i]["v_scales"][:, g, :],
-                in_=v_grouped[g][:],
+                in_=v_grouped[(i, g)][:],
             )
 
         def multiply(i, tb):
@@ -262,74 +365,135 @@ def tile_nucleusxmultiscaleretention_pb_t_kernel(tc, qr, kr, v, decay_mask, out)
                 )
             st["acc"][tb] = acc
 
-        def store(i, tb):
+        def store(copy, i, tb):
             b, h = heads[i]
             result = results.tile([P, HD], F32, tag="result", name="result")
-            nc.scalar.copy(out=result[:], in_=state[i]["acc"][tb][:])
+            copy(out=result[:], in_=state[i]["acc"][tb][:])
             nc.sync.dma_start(out=out[b, h, tb * P : (tb + 1) * P, :], in_=result[:])
 
-        new_head(0)
-        turn_rows(0, "q")
-        turn_rows(0, "k")
-        keep_turned(0, "q")
-        keep_turned(0, "k")
-        for tb in range(SCORES_AHEAD):
+        vec, sca = nc.vector.tensor_copy, nc.scalar.copy
+
+        def keep_half(copy, i, key, c):
+            if c == 0:
+                state[i][key + "T"] = per_head.tile([P, T], BF16, tag=key + "T", name=key + "T")
+            rows = {"q": q_rows, "k": k_rows}[key][(i, c)]
+            bank = psum.tile([P, BLOCKS_PER_CHUNK, P], BF16, tag="bank", name="qk_bank")
+            for n in range(BLOCKS_PER_CHUNK):
+                nc.tensor.transpose(bank[:, n, :], rows[:, n, :], ident_bf[:])
+            copy(out=state[i][key + "T"][:, c * K_PASS:(c + 1) * K_PASS], in_=bank[:].rearrange("d n t -> d (n t)"))
+
+        keep_half(vec, 0, "q", 0)
+        keep_half(sca, 0, "k", 0)
+        for tb in range(PREFETCH):
             scores(0, tb)
 
-        for i in range(n_heads + 1):
-            j = i - 1
-            masking = i < n_heads
-            finishing = j >= 0
-            if i + 2 < n_heads:
-                load_head(i + 2)
 
-            for step in range(TB + REGROUP_BEHIND):
-                if masking and step + SCORES_AHEAD < TB:
+        for i in range(n_heads):
+            j = i - 1
+            finishing = j >= 0
+            last = i == n_heads - 1
+            nxt = i + 3
+            if nxt < n_heads:
+                load_rows(nxt, 0)
+                load_rows(nxt, 1)
+            if i == 1:
+                for pair in range(4):
+                    load_mask(1, pair)
+            if 2 <= i + 2 < n_heads:
+                load_v(i + 2, 1)
+                load_v(i + 2, 0)
+            late = [tb for tb in range(TB) if tb not in early(j)] if finishing else []
+            for step in range(max(TB, len(late) + REGROUP_BEHIND)):
+                if PREFETCH <= step + SCORES_AHEAD < TB:
                     scores(i, step + SCORES_AHEAD)
+                if i == 0 and step == 1:
+                    keep_half(sca, 0, "q", 1)
+                    keep_half(sca, 0, "k", 1)
                 if i + 1 < n_heads:
                     if step == TURN_QK_STEP:
-                        new_head(i + 1)
-                        turn_rows(i + 1, "q")
+                        turn_all(i + 1, "q")
                     if step == TURN_QK_STEP + 1:
-                        turn_rows(i + 1, "k")
-                        keep_turned(i + 1, "q")
+                        turn_all(i + 1, "k")
+                        keep_turned(sca, i + 1, "q")
                     if step == TURN_QK_STEP + 2:
-                        keep_turned(i + 1, "k")
-                if finishing and step < TB:
-                    scale_rows(j, step, vector_is_free=not masking)
-                if masking and step < TB:
+                        keep_turned(sca, i + 1, "k")
+                for (h, g, n0, n1) in G_WORK(i).get(step, ()):
+                    regroup_v(gps, h, g, n0, n1)
+                if step < len(late):
+                    scale_rows(nc.gpsimd, j, late[step])
+                if step < TB:
                     mask_scores(i, step)
-                if finishing and 0 <= step - TURN_BEHIND < TB:
-                    turn_p(j, step - TURN_BEHIND)
-                if finishing and 0 <= step - REGROUP_BEHIND < TB:
-                    regroup_p(j, step - REGROUP_BEHIND)
-                if masking and 0 <= step - V_ON_SCALAR_STEP < V_PIECES:
-                    piece = step - V_ON_SCALAR_STEP
-                    regroup_v(
-                        nc.scalar.copy, i, 1, piece * HD // V_PIECES, (piece + 1) * HD // V_PIECES
-                    )
-
+                if 0 <= step - TURN_BEHIND < len(late):
+                    turn_p(j, late[step - TURN_BEHIND])
+                if 0 <= step - REGROUP_BEHIND < len(late):
+                    tb = late[step - REGROUP_BEHIND]
+                    regroup_p(vec if tb in V_REGROUPS(i) else sca, j, tb)
+                for (h, g, n0, n1) in S_WORK(i).get(step, ()):
+                    regroup_v(sca, h, g, n0, n1)
+                if i == 0 and step == TM0:
+                    turn_mask(0, 0)
+                    turn_mask(0, 1)
+            for tb in early(i):
+                turn_p(i, tb)
+            if 2 <= i <= 3:
+                turn_mask(1, i - 2)
             if i + 1 < n_heads:
-                for tb in range(SCORES_AHEAD):
+                for tb in range(PREFETCH):
                     scores(i + 1, tb)
-            if masking:
-                join_row_sums(i)
-            if finishing:
-                for tb in range(QUANTISED_FIRST):
-                    quantise_p(tb)
-            if masking:
-                regroup_v(nc.vector.tensor_copy, i, 0, 0, HD)
-            if finishing:
-                for tb in range(QUANTISED_FIRST, TB):
-                    quantise_p(tb)
-            if masking:
-                clip_row_sums(i)
-                quantise_v(i, 0)
+            for tb in early(i):
+                regroup_p(sca, i, tb)
+            if i + 1 < n_heads and early(i + 1):
+                early_sums(i + 1)
+            join_row_sums(i)
+            if i == 0:
+                clip_row_sums()
                 invert_row_sums(i)
-                quantise_v(i, 1)
-            if finishing:
-                for tb in range(TB + 1):
-                    if tb < TB:
-                        multiply(j, tb)
-                    if tb > 0:
-                        store(j, tb - 1)
+                continue
+            if i == 1:
+                quantise_v(0, 0)
+                quantise_v(0, 1)
+            for tb in range(QUANTISED_FIRST):
+                quantise_p(j, tb)
+            if last:
+                clip_row_sums()
+            for (h, g, n0, n1) in V_WORK(i):
+                regroup_v(vec, h, g, n0, n1)
+            for tb in range(QUANTISED_FIRST, TB):
+                if last and tb == 4:
+                    invert_row_sums(i)
+                quantise_p(j, tb)
+            if not last and early(i + 1):
+                early_sums2(i + 1)
+            quantise_v(i, 0)
+            if not last:
+                clip_row_sums()
+            quantise_v(i, 1)
+            if not last:
+                invert_row_sums(i)
+            for tb in range(TB + 1):
+                if tb < TB:
+                    multiply(j, tb)
+                if tb > 0:
+                    store(sca, j, tb - 1)
+
+        j = n_heads - 1
+        order = (6,7,0,1,2,3,4,5)
+        n = len(order)
+        for step in range(n + 6):
+            if step < n:
+                tb = order[step]
+                if tb not in EARLY:
+                    scale_rows(nc.vector, j, tb)
+            if 0 <= step - 1 < n and order[step - 1] not in EARLY:
+                turn_p(j, order[step - 1])
+            if 0 <= step - 2 < n:
+                tb = order[step - 2]
+                if tb not in EARLY:
+                    regroup_p(vec if tb in (0,1,3,5) else sca, j, tb)
+            if 0 <= step - 3 < n:
+                quantise_p(j, order[step - 3])
+            if 0 <= step - 4 < n:
+                multiply(j, order[step - 4])
+            if 0 <= step - 5 < n:
+                tb = order[step - 5]
+                store(vec if tb in (0,2,4,6) else sca, j, tb)

@@ -30,7 +30,7 @@ def V_REGROUPS(i):
 def G_WORK(i):
     if i <= 2:
         return {}
-    return {6: [(i, 1, 0, 512)]}
+    return {6: [(i, 1, 0, 256)]}
 def S_WORK(i):
     if i == 0:
         return {7: [(0, 1, 0, 512)]}
@@ -38,13 +38,13 @@ def S_WORK(i):
         return {0: [(0, 0, 0, 256)], 3: [(0, 0, 256, 512)], 10: [(1, 1, 256, 512)]}
     if i == 2:
         return {3: [(2, 1, 128, 512)]}
-    return {3: [(i, 1, 512, 512)] if 512 < 512 else [], 4: [(i, 0, 320, 512)] if 192 else []}
+    return {3: [(i, 1, 256, 512)] if 256 < 512 else [], 4: [(i, 0, 512, 512)] if 0 else []}
 def V_WORK(i):
     if i == 1:
         return [(i, 0, 0, 512), (i, 1, 0, 256)]
     if i == 2:
         return [(i, 0, 0, 512), (i, 1, 0, 128)]
-    return [(i, 0, 0, 320)]
+    return [(i, 0, 0, 512)]
 
 SCORES_AHEAD = 2
 TURN_BEHIND = 2
@@ -336,6 +336,15 @@ def tile_nucleusxmultiscaleretention_pb_t_kernel(tc, qr, kr, v, decay_mask, out)
                 in_=v_rows[(i, g)][:, :, n0:n1].rearrange("p j (c i) -> p c j i", i=4),
             )
 
+        def regroup_v_gpsimd(i, g, n0, n1):
+            if (i, g) not in v_grouped:
+                v_grouped[(i, g)] = per_head.tile([P, HD * PACK], BF16, tag="v_grouped%d" % g, name="v_grouped", align_bytes=64)
+            nc.gpsimd.tensor_scalar(
+                out=v_grouped[(i, g)][:, n0 * PACK : n1 * PACK].rearrange("p (n j) -> p n j", j=PACK),
+                in0=v_rows[(i, g)][:, :, n0:n1].rearrange("p j n -> p n j"),
+                scalar1=1.0, scalar2=0.0, op0=MULT, op1=mybir.AluOpType.add,
+            )
+
         def quantise_v(i, g):
             if g == 0:
                 state[i]["v_codes"] = per_head.tile(
@@ -418,7 +427,7 @@ def tile_nucleusxmultiscaleretention_pb_t_kernel(tc, qr, kr, v, decay_mask, out)
                     if step == TURN_QK_STEP + 2:
                         keep_turned(sca, i + 1, "k")
                 for (h, g, n0, n1) in G_WORK(i).get(step, ()):
-                    regroup_v(gps, h, g, n0, n1)
+                    regroup_v_gpsimd(h, g, n0, n1)
                 if step < len(late):
                     scale_rows(nc.gpsimd, j, late[step])
                 if step < TB:

@@ -22,28 +22,26 @@ PSUM_BANKS = 8
 
 EARLY = (6, 7)
 PREFETCH = 3
-FIRST_EARLY = 2
+FIRST_EARLY = 99
 TM0 = 7
 V_VECTOR = 0
 def V_REGROUPS(i):
     return ()
 def G_WORK(i):
-    if i <= 2:
-        return {}
-    return {6: [(i, 1, 0, 256)]}
+    return {}
 def S_WORK(i):
     if i == 0:
         return {7: [(0, 1, 0, 512)]}
     if i == 1:
-        return {0: [(0, 0, 0, 256)], 3: [(0, 0, 256, 512)], 10: [(1, 1, 256, 512)]}
-    if i == 2:
-        return {3: [(2, 1, 128, 512)]}
-    return {3: [(i, 1, 256, 512)] if 256 < 512 else [], 4: [(i, 0, 512, 512)] if 0 else []}
+        return {0: [(0, 0, 0, 256)], 3: [(0, 0, 256, 512)], 10: [(1, 1, 192, 512)]}
+    if i == 7:
+        return {3: [(i, 1, 0, 256)], 4: [(i, 1, 256, 512)], 5: [(i, 0, 256, 512)]}
+    return {3: [(i, 1, 0, 288)], 4: [(i, 1, 288, 512)]}
 def V_WORK(i):
     if i == 1:
-        return [(i, 0, 0, 512), (i, 1, 0, 256)]
-    if i == 2:
-        return [(i, 0, 0, 512), (i, 1, 0, 128)]
+        return [(i, 0, 0, 512), (i, 1, 0, 192)]
+    if i == 7:
+        return [(i, 0, 0, 256)]
     return [(i, 0, 0, 512)]
 
 SCORES_AHEAD = 2
@@ -73,7 +71,7 @@ def tile_nucleusxmultiscaleretention_pb_t_kernel(tc, qr, kr, v, decay_mask, out)
         results = ctx.enter_context(tc.tile_pool(name="results", bufs=TB))
         r_pool = ctx.enter_context(tc.tile_pool(name="r_pool", bufs=2))
         rows_pool = ctx.enter_context(tc.tile_pool(name="rows_pool", bufs=4))
-        r_once = ctx.enter_context(tc.tile_pool(name="r_once", bufs=1))
+        r_once = ctx.enter_context(tc.tile_pool(name="r_once", bufs=2))
         mt_pool = ctx.enter_context(tc.tile_pool(name="mt_pool", bufs=1))
         psum = ctx.enter_context(tc.psum_pool(name="psum", bufs=PSUM_BANKS))
         ctx.enter_context(tc.manual_schedule())
@@ -440,11 +438,10 @@ def tile_nucleusxmultiscaleretention_pb_t_kernel(tc, qr, kr, v, decay_mask, out)
                 for (h, g, n0, n1) in S_WORK(i).get(step, ()):
                     regroup_v(sca, h, g, n0, n1)
                 if i == 0 and step == TM0:
-                    turn_mask(0, 0)
-                    turn_mask(0, 1)
+                    pass
             for tb in early(i):
                 turn_p(i, tb)
-            if 2 <= i <= 3:
+            if False:
                 turn_mask(1, i - 2)
             if i + 1 < n_heads:
                 for tb in range(PREFETCH):
@@ -453,8 +450,8 @@ def tile_nucleusxmultiscaleretention_pb_t_kernel(tc, qr, kr, v, decay_mask, out)
                 regroup_p(sca, i, tb)
             if i + 1 < n_heads and early(i + 1):
                 early_sums(i + 1)
-            join_row_sums(i)
             if i == 0:
+                join_row_sums(i)
                 clip_row_sums()
                 invert_row_sums(i)
                 continue
@@ -463,6 +460,7 @@ def tile_nucleusxmultiscaleretention_pb_t_kernel(tc, qr, kr, v, decay_mask, out)
                 quantise_v(0, 1)
             for tb in range(QUANTISED_FIRST):
                 quantise_p(j, tb)
+            join_row_sums(i)
             if last:
                 clip_row_sums()
             for (h, g, n0, n1) in V_WORK(i):
@@ -486,18 +484,18 @@ def tile_nucleusxmultiscaleretention_pb_t_kernel(tc, qr, kr, v, decay_mask, out)
                     store(sca, j, tb - 1)
 
         j = n_heads - 1
-        order = (6,7,0,1,2,3,4,5)
+        order = (0,1,2,3,4,5,6,7)
         n = len(order)
         for step in range(n + 6):
             if step < n:
                 tb = order[step]
-                if tb not in EARLY:
+                if tb not in ():
                     scale_rows(nc.vector, j, tb)
-            if 0 <= step - 1 < n and order[step - 1] not in EARLY:
+            if 0 <= step - 1 < n and order[step - 1] not in ():
                 turn_p(j, order[step - 1])
             if 0 <= step - 2 < n:
                 tb = order[step - 2]
-                if tb not in EARLY:
+                if tb not in ():
                     regroup_p(vec if tb in (0,1,3,5) else sca, j, tb)
             if 0 <= step - 3 < n:
                 quantise_p(j, order[step - 3])

@@ -26,20 +26,21 @@ FIRST_EARLY = 99
 TM0 = 7
 V_VECTOR = 0
 def V_REGROUPS(i):
-    return ()
+    return (3,)
+SCALAR_SCALES = (1,)
 def G_WORK(i):
     return {}
 def S_WORK(i):
     if i == 0:
         return {7: [(0, 1, 0, 512)]}
     if i == 1:
-        return {0: [(0, 0, 0, 256)], 3: [(0, 0, 256, 512)], 10: [(1, 1, 192, 512)]}
+        return {0: [(0, 0, 0, 256)], 3: [(0, 0, 256, 512)], 10: [(1, 1, 96, 512)]}
     if i == 7:
         return {3: [(i, 1, 0, 256)], 4: [(i, 1, 256, 512)], 5: [(i, 0, 256, 512)]}
     return {3: [(i, 1, 0, 288)], 4: [(i, 1, 288, 512)]}
 def V_WORK(i):
     if i == 1:
-        return [(i, 0, 0, 512), (i, 1, 0, 192)]
+        return [(i, 0, 0, 512), (i, 1, 0, 96)]
     if i == 7:
         return [(i, 0, 0, 256)]
     return [(i, 0, 0, 512)]
@@ -73,6 +74,7 @@ def tile_nucleusxmultiscaleretention_pb_t_kernel(tc, qr, kr, v, decay_mask, out)
         rows_pool = ctx.enter_context(tc.tile_pool(name="rows_pool", bufs=4))
         r_once = ctx.enter_context(tc.tile_pool(name="r_once", bufs=2))
         mt_pool = ctx.enter_context(tc.tile_pool(name="mt_pool", bufs=1))
+        pair_results = ctx.enter_context(tc.tile_pool(name="pair_results", bufs=4))
         psum = ctx.enter_context(tc.psum_pool(name="psum", bufs=PSUM_BANKS))
         ctx.enter_context(tc.manual_schedule())
 
@@ -231,7 +233,8 @@ def tile_nucleusxmultiscaleretention_pb_t_kernel(tc, qr, kr, v, decay_mask, out)
             if not is_early:
                 r_sb = (r_once if tb in EARLY else r_pool).tile([P, (tb + 1) * P], F32, tag="r%d" % tb, name="r%d" % tb)
                 st["r"][tb] = r_sb
-            for g, bank in enumerate(st["scores"][tb]):
+            for g in reversed(range(len(st["scores"][tb]))):
+                bank = st["scores"][tb][g]
                 lo = g * K_PASS
                 hi = min((tb + 1) * P, lo + K_PASS)
                 if is_early:
@@ -378,6 +381,15 @@ def tile_nucleusxmultiscaleretention_pb_t_kernel(tc, qr, kr, v, decay_mask, out)
             copy(out=result[:], in_=state[i]["acc"][tb][:])
             nc.sync.dma_start(out=out[b, h, tb * P : (tb + 1) * P, :], in_=result[:])
 
+        def store_pair(copy, i, tb):
+            b, h = heads[i]
+            result = pair_results.tile([P, 2, HD], F32, tag="result2", name="result2")
+            for n in (1, 0):
+                copy(out=result[:, n, :], in_=state[i]["acc"][tb - 1 + n][:])
+            nc.sync.dma_start(
+                out=out[b, h, (tb - 1) * P : (tb + 1) * P, :].rearrange("(n p) d -> p n d", p=P), in_=result[:]
+            )
+
         vec, sca = nc.vector.tensor_copy, nc.scalar.copy
 
         def keep_half(copy, i, key, c):
@@ -426,7 +438,13 @@ def tile_nucleusxmultiscaleretention_pb_t_kernel(tc, qr, kr, v, decay_mask, out)
                         keep_turned(sca, i + 1, "k")
                 for (h, g, n0, n1) in G_WORK(i).get(step, ()):
                     regroup_v_gpsimd(h, g, n0, n1)
-                if step < len(late):
+                for tb in SCALAR_SCALES:
+                    if finishing and step == max(tb - 2, 0):
+                        nc.scalar.activation(
+                            out=p_of(j, tb)[:, : (tb + 1) * P], in_=state[j]["r"][tb][:],
+                            func=mybir.ActivationFunctionType.Copy, scale=state[j]["inverse"][tb],
+                        )
+                if step < len(late) and late[step] not in SCALAR_SCALES:
                     scale_rows(nc.gpsimd, j, late[step])
                 if step < TB:
                     mask_scores(i, step)
@@ -480,8 +498,8 @@ def tile_nucleusxmultiscaleretention_pb_t_kernel(tc, qr, kr, v, decay_mask, out)
             for tb in range(TB + 1):
                 if tb < TB:
                     multiply(j, tb)
-                if tb > 0:
-                    store(sca, j, tb - 1)
+                if tb > 0 and tb % 2 == 0:
+                    store_pair(sca, j, tb - 1)
 
         j = n_heads - 1
         order = (0,1,2,3,4,5,6,7)
@@ -503,4 +521,4 @@ def tile_nucleusxmultiscaleretention_pb_t_kernel(tc, qr, kr, v, decay_mask, out)
                 multiply(j, order[step - 4])
             if 0 <= step - 5 < n:
                 tb = order[step - 5]
-                store(vec if tb in (0,2,4,6) else sca, j, tb)
+                store(vec if tb in (3, 5, 7) else sca, j, tb)

from contextlib import ExitStack

import concourse.mybir as mybir
from concourse.masks import make_identity

F32 = mybir.dt.float32
BF16 = mybir.dt.bfloat16
U32 = mybir.dt.uint32
U8 = mybir.dt.uint8
FP8X4 = mybir.dt.float8_e4m3fn_x4
MULT = mybir.AluOpType.mult
MAX = mybir.AluOpType.max

B, NH, T, KD, HD = 4, 2, 1024, 128, 512
P = 128
PACK = 4
K_PASS = P * PACK
TB = T // P
BLOCKS_PER_CHUNK = K_PASS // P
N_PASSES = T // K_PASS
PSUM_BANKS = 8

EARLY = (6, 7)
PREFETCH = 3
FIRST_EARLY = 99
TM0 = 7
V_VECTOR = 0
def V_REGROUPS(i):
    return (3,)
SCALAR_SCALES = (1,)
def G_WORK(i):
    return {}
def S_WORK(i):
    if i == 0:
        return {7: [(0, 1, 0, 512)]}
    if i == 1:
        return {0: [(0, 0, 0, 256)], 3: [(0, 0, 256, 512)], 10: [(1, 1, 96, 512)]}
    if i == 7:
        return {3: [(i, 1, 0, 256)], 4: [(i, 1, 256, 512)], 5: [(i, 0, 256, 512)]}
    return {3: [(i, 1, 0, 288)], 4: [(i, 1, 288, 512)]}
def V_WORK(i):
    if i == 1:
        return [(i, 0, 0, 512), (i, 1, 0, 96)]
    if i == 7:
        return [(i, 0, 0, 256)]
    return [(i, 0, 0, 512)]

SCORES_AHEAD = 2
TURN_BEHIND = 2
REGROUP_BEHIND = 3
TURN_QK_STEP = TB - 1 - SCORES_AHEAD
V_ON_SCALAR_STEP = REGROUP_BEHIND
V_PIECES = 2
VECTOR_REGROUPS = TB - REGROUP_BEHIND
QUANTISED_FIRST = 2

FLOPS = 2 * B * NH * sum(K_PASS * K_PASS * (c + 1) for c in range(N_PASSES)) * (KD + HD)


def passes_of(tb):
    return tb // BLOCKS_PER_CHUNK + 1


def tile_nucleusxmultiscaleretention_pb_t_kernel(tc, qr, kr, v, decay_mask, out):
    nc = tc.nc
    heads = [(b, h) for h in range(NH) for b in range(B)]
    n_heads = len(heads)

    with ExitStack() as ctx:
        fixed = ctx.enter_context(tc.tile_pool(name="fixed", bufs=1))
        per_head = ctx.enter_context(tc.tile_pool(name="per_head", bufs=2))
        results = ctx.enter_context(tc.tile_pool(name="results", bufs=TB))
        r_pool = ctx.enter_context(tc.tile_pool(name="r_pool", bufs=2))
        rows_pool = ctx.enter_context(tc.tile_pool(name="rows_pool", bufs=4))
        r_once = ctx.enter_context(tc.tile_pool(name="r_once", bufs=2))
        mt_pool = ctx.enter_context(tc.tile_pool(name="mt_pool", bufs=1))
        pair_results = ctx.enter_context(tc.tile_pool(name="pair_results", bufs=4))
        psum = ctx.enter_context(tc.psum_pool(name="psum", bufs=PSUM_BANKS))
        ctx.enter_context(tc.manual_schedule())

        q_rows, k_rows, v_rows, mask_tiles = {}, {}, {}, {}

        def load_rows(i, c):
            b, h = heads[i]
            for key, kept, dram in (("q", q_rows, qr), ("k", k_rows, kr)):
                sb = rows_pool.tile([P, BLOCKS_PER_CHUNK, KD], BF16, tag=key + "_rows%d" % c, name=key + "_rows")
                nc.sync.dma_start(
                    out=sb[:],
                    in_=dram[b, h, c * K_PASS : (c + 1) * K_PASS].rearrange("(n p) d -> p n d", p=P),
                )
                kept[(i, c)] = sb

        def load_mask(h, pair):
            keys = 2 * (pair + 1) * P
            mask = fixed.tile([P, 2, keys], BF16, name="mask%d_%d" % (h, pair))
            nc.sync.dma_start(
                out=mask[:],
                in_=decay_mask[0, h, 2 * pair * P : 2 * (pair + 1) * P, 0:keys].rearrange(
                    "(n p) s -> p n s", p=P
                ),
            )
            mask_tiles[(h, pair)] = mask

        def load_v(i, g):
            b, h = heads[i]
            v_sb = rows_pool.tile([P, PACK, HD], BF16, tag="v_rows%d" % g, name="v_rows")
            nc.sync.dma_start(
                out=v_sb[:].rearrange("p (u e) n -> p u (e n)", e=2),
                in_=v[b, h, g * K_PASS : (g + 1) * K_PASS].rearrange("(a p e) n -> p a (e n)", p=P, e=2),
            )
            v_rows[(i, g)] = v_sb

        load_rows(0, 0)
        load_mask(0, 0)
        load_rows(0, 1)
        load_mask(0, 1)
        load_mask(0, 2)
        load_mask(0, 3)
        load_rows(1, 0)
        load_rows(1, 1)
        load_v(0, 1)
        load_v(0, 0)
        load_rows(2, 0)
        load_rows(2, 1)
        load_v(1, 1)
        load_v(1, 0)

        ident_bf = fixed.tile([P, P], BF16, name="ident_bf")
        make_identity(nc, ident_bf[:])
        ident_f32 = fixed.tile([P, P], F32, name="ident_f32")
        make_identity(nc, ident_f32[:])

        p_sb, p_codes, p_scales, p_grouped = [], [], [], {}
        for tb in range(TB):
            width = K_PASS * passes_of(tb)
            p_sb.append([])
            for n in range(2 if tb in EARLY else 1):
                p_tile = fixed.tile([P, width], BF16, name="p_sb%d_%d" % (tb, n))
                if (tb + 1) * P < width:
                    nc.vector.memset(p_tile[:, (tb + 1) * P :], 0.0)
                p_sb[tb].append(p_tile)
            p_codes.append(
                fixed.tile([P, width // PACK], U32, name="p_codes%d" % tb, align_bytes=64)
            )
            p_scales.append(
                fixed.tile([P, width // PACK], U8, name="p_scales%d" % tb, align_bytes=64)
            )
        v_grouped = {}
        row_sums = fixed.tile([P, TB + len(EARLY), 2], F32, name="row_sums")
        nc.vector.memset(row_sums[:], 1.0)
        unread = fixed.tile([P, KD], F32, name="unread")
        mask_turned = {}

        def early(i):
            return EARLY if i >= FIRST_EARLY else ()

        def turn_mask(h, e):
            if e == 0:
                mask_turned[h] = mt_pool.tile([P, len(EARLY), TB, P], BF16, tag="mask_turned%d" % h, name="mask_turned")
            turned = mask_turned[h]
            tb = EARLY[e]
            bank = psum.tile([P, TB, P], BF16, tag="bank", name="mask_bank")
            for sb in range(tb + 1):
                nc.tensor.transpose(
                    bank[:, sb, :], mask_tiles[(h, tb // 2)][:, tb % 2, sb * P : (sb + 1) * P], ident_bf[:]
                )
            nc.scalar.copy(out=turned[:, e, : tb + 1, :].rearrange("s n t -> s (n t)"), in_=bank[:, : tb + 1, :].rearrange("s n t -> s (n t)"))

        def early_sums(i):
            bank = psum.tile([P, len(EARLY), KD], F32, tag="bank", name="mk_bank")
            turned = mask_turned[heads[i][1]]
            for e, tb in enumerate(EARLY):
                for sb in range(tb + 1):
                    nc.tensor.matmul(
                        bank[:, e, :],
                        lhsT=turned[:, e, sb, :],
                        rhs=k_rows[(i, sb // BLOCKS_PER_CHUNK)][:, sb % BLOCKS_PER_CHUNK, :],
                        start=(sb == 0),
                        stop=(sb == tb),
                    )
            state[i]["mk_bank"] = bank

        def early_sums2(i):
            for e, tb in enumerate(EARLY):
                nc.vector.scalar_tensor_tensor(
                    out=unread[:],
                    in0=state[i]["mk_bank"][:, e, :],
                    scalar=1.0,
                    in1=q_rows[(i, tb // BLOCKS_PER_CHUNK)][:, tb % BLOCKS_PER_CHUNK, :],
                    op0=MULT,
                    op1=MULT,
                    accum_out=row_sums[:, TB + e, 0:1],
                )

        state = {}
        gps = lambda out, in_: nc.gpsimd.tensor_scalar(out=out, in0=in_, scalar1=1.0, scalar2=0.0, op0=MULT, op1=mybir.AluOpType.add)
        for i in range(n_heads):
            state[i] = {"scores": {}, "r": {}, "p_bank": {}, "acc": {}, "inverse": {}, "second_sums": {}}

        def turn_all(i, key):
            rows = {"q": q_rows, "k": k_rows}[key]
            bank = psum.tile([P, TB, P], BF16, tag="bank", name="qk_bank")
            for n in range(TB):
                nc.tensor.transpose(bank[:, n, :], rows[(i, n // BLOCKS_PER_CHUNK)][:, n % BLOCKS_PER_CHUNK, :], ident_bf[:])
            state[i][key + "_bank"] = bank

        def keep_turned(copy, i, key):
            turned = per_head.tile([P, T], BF16, tag=key + "T", name=key + "T")
            copy(out=turned[:], in_=state[i][key + "_bank"][:].rearrange("d n t -> d (n t)"))
            state[i][key + "T"] = turned

        def scores(i, tb):
            st = state[i]
            banks = []
            for g in range(passes_of(tb)):
                lo = g * K_PASS
                hi = min((tb + 1) * P, lo + K_PASS)
                bank = psum.tile([P, K_PASS], F32, tag="bank", name="score_bank")
                nc.tensor.matmul(
                    bank[:, : hi - lo],
                    lhsT=st["qT"][:, tb * P : (tb + 1) * P],
                    rhs=st["kT"][:, lo:hi],
                    start=True,
                    stop=True,
                )
                banks.append(bank)
            st["scores"][tb] = banks

        def mask_scores(i, tb):
            st = state[i]
            mask = mask_tiles[(heads[i][1], tb // 2)]
            is_early = tb in early(i)
            if not is_early:
                r_sb = (r_once if tb in EARLY else r_pool).tile([P, (tb + 1) * P], F32, tag="r%d" % tb, name="r%d" % tb)
                st["r"][tb] = r_sb
            for g in reversed(range(len(st["scores"][tb]))):
                bank = st["scores"][tb][g]
                lo = g * K_PASS
                hi = min((tb + 1) * P, lo + K_PASS)
                if is_early:
                    nc.vector.scalar_tensor_tensor(
                        out=p_of(i, tb)[:, lo:hi],
                        in0=bank[:, : hi - lo],
                        scalar=st["inverse"][tb],
                        in1=mask[:, tb % 2, lo:hi],
                        op0=MULT,
                        op1=MULT,
                    )
                else:
                    if g == 0:
                        row_sum = row_sums[:, tb, 0:1]
                    else:
                        row_sum = second_sums[:, tb - BLOCKS_PER_CHUNK : tb - BLOCKS_PER_CHUNK + 1]
                    nc.vector.scalar_tensor_tensor(
                        out=r_sb[:, lo:hi],
                        in0=bank[:, : hi - lo],
                        scalar=1.0,
                        in1=mask[:, tb % 2, lo:hi],
                        op0=MULT,
                        op1=MULT,
                        accum_out=row_sum,
                    )

        second_sums = fixed.tile([P, BLOCKS_PER_CHUNK], F32, name="second_sums")

        def join_row_sums(i):
            n = TB - BLOCKS_PER_CHUNK - len(early(i))
            first = row_sums[:, BLOCKS_PER_CHUNK : BLOCKS_PER_CHUNK + n, 0]
            nc.vector.tensor_add(out=first, in0=first, in1=second_sums[:, :n])

        denom = {}

        def clip_row_sums():
            denom[0] = per_head.tile([P, TB + len(EARLY)], F32, tag="denom", name="denom")
            nc.vector.tensor_reduce(
                out=denom[0][:],
                in_=row_sums[:],
                op=MAX,
                axis=mybir.AxisListType.X,
                apply_absolute_value=True,
            )

        def invert_row_sums(i):
            inverse = per_head.tile([P, TB + len(EARLY)], F32, tag="inverse", name="inverse")
            nc.vector.reciprocal(out=inverse[:], in_=denom[0][:])
            for tb in range(TB):
                if tb not in early(i):
                    state[i]["inverse"][tb] = inverse[:, tb : tb + 1]
            if i + 1 < n_heads and early(i + 1):
                for e, tb in enumerate(EARLY):
                    state[i + 1]["inverse"][tb] = inverse[:, TB + e : TB + e + 1]

        def p_of(i, tb):
            return p_sb[tb][i % len(p_sb[tb])]

        def scale_rows(engine, i, tb):
            st = state[i]
            p_live = p_of(i, tb)[:, : (tb + 1) * P]
            inverse = st["inverse"][tb]
            engine.tensor_scalar(
                out=p_live, in0=st["r"][tb][:], scalar1=inverse, scalar2=1.0, op0=MULT, op1=MULT
            )

        def turn_p(i, tb):
            words = p_of(i, tb)[:].bitcast(F32)
            p_bank = psum.tile([P, passes_of(tb), 2, P], F32, tag="bank", name="p_bank")
            for g in range(passes_of(tb)):
                for u in range(2):
                    w0 = (2 * g + u) * P
                    nc.tensor.transpose(p_bank[:, g, u, :], words[:, w0 : w0 + P], ident_f32[:])
            state[i]["p_bank"][tb] = p_bank

        def regroup_p(copy, i, tb):
            p_grouped[tb] = per_head.tile([P, K_PASS * passes_of(tb)], BF16, tag="p_grouped%d" % tb, name="p_grouped", align_bytes=64)
            p_kept[(i, tb)] = p_grouped[tb]
            copy(
                out=p_grouped[tb][:]
                .bitcast(F32)
                .rearrange("p (g t u) -> p g t u", g=passes_of(tb), u=2),
                in_=state[i]["p_bank"][tb][:].rearrange("p g u t -> p g t u"),
            )

        p_kept = {}

        def quantise_p(i, tb):
            nc.vector.quantize_mx(
                out=p_codes[tb][:].bitcast(FP8X4), scales=p_scales[tb][:], in_=p_kept[(i, tb)][:]
            )

        def regroup_v(copy, i, g, n0, n1):
            if (i, g) not in v_grouped:
                v_grouped[(i, g)] = per_head.tile([P, HD * PACK], BF16, tag="v_grouped%d" % g, name="v_grouped", align_bytes=64)
            copy(
                out=v_grouped[(i, g)][:, n0 * PACK : n1 * PACK].rearrange(
                    "p (c i j) -> p c j i", i=4, j=PACK
                ),
                in_=v_rows[(i, g)][:, :, n0:n1].rearrange("p j (c i) -> p c j i", i=4),
            )

        def regroup_v_gpsimd(i, g, n0, n1):
            if (i, g) not in v_grouped:
                v_grouped[(i, g)] = per_head.tile([P, HD * PACK], BF16, tag="v_grouped%d" % g, name="v_grouped", align_bytes=64)
            nc.gpsimd.tensor_scalar(
                out=v_grouped[(i, g)][:, n0 * PACK : n1 * PACK].rearrange("p (n j) -> p n j", j=PACK),
                in0=v_rows[(i, g)][:, :, n0:n1].rearrange("p j n -> p n j"),
                scalar1=1.0, scalar2=0.0, op0=MULT, op1=mybir.AluOpType.add,
            )

        def quantise_v(i, g):
            if g == 0:
                state[i]["v_codes"] = per_head.tile(
                    [P, N_PASSES, HD], U32, tag="v_codes", name="v_codes", align_bytes=64
                )
                state[i]["v_scales"] = per_head.tile(
                    [P, N_PASSES, HD], U8, tag="v_scales", name="v_scales", align_bytes=64
                )
            nc.vector.quantize_mx(
                out=state[i]["v_codes"][:, g, :].bitcast(FP8X4),
                scales=state[i]["v_scales"][:, g, :],
                in_=v_grouped[(i, g)][:],
            )

        def multiply(i, tb):
            st = state[i]
            acc = psum.tile([P, HD], F32, tag="bank", name="acc")
            for g in range(passes_of(tb)):
                nc.tensor.matmul_mx(
                    out=acc[:],
                    lhsT=p_codes[tb][:, g * P : (g + 1) * P].bitcast(FP8X4),
                    lhsT_scale=p_scales[tb][:, g * P : (g + 1) * P],
                    rhs=st["v_codes"][:, g, :].bitcast(FP8X4),
                    rhs_scale=st["v_scales"][:, g, :],
                    start=(g == 0),
                    stop=(g == passes_of(tb) - 1),
                )
            st["acc"][tb] = acc

        def store(copy, i, tb):
            b, h = heads[i]
            result = results.tile([P, HD], F32, tag="result", name="result")
            copy(out=result[:], in_=state[i]["acc"][tb][:])
            nc.sync.dma_start(out=out[b, h, tb * P : (tb + 1) * P, :], in_=result[:])

        def store_pair(copy, i, tb):
            b, h = heads[i]
            result = pair_results.tile([P, 2, HD], F32, tag="result2", name="result2")
            for n in (1, 0):
                copy(out=result[:, n, :], in_=state[i]["acc"][tb - 1 + n][:])
            nc.sync.dma_start(
                out=out[b, h, (tb - 1) * P : (tb + 1) * P, :].rearrange("(n p) d -> p n d", p=P), in_=result[:]
            )

        vec, sca = nc.vector.tensor_copy, nc.scalar.copy

        def keep_half(copy, i, key, c):
            if c == 0:
                state[i][key + "T"] = per_head.tile([P, T], BF16, tag=key + "T", name=key + "T")
            rows = {"q": q_rows, "k": k_rows}[key][(i, c)]
            bank = psum.tile([P, BLOCKS_PER_CHUNK, P], BF16, tag="bank", name="qk_bank")
            for n in range(BLOCKS_PER_CHUNK):
                nc.tensor.transpose(bank[:, n, :], rows[:, n, :], ident_bf[:])
            copy(out=state[i][key + "T"][:, c * K_PASS:(c + 1) * K_PASS], in_=bank[:].rearrange("d n t -> d (n t)"))

        keep_half(vec, 0, "q", 0)
        keep_half(sca, 0, "k", 0)
        for tb in range(PREFETCH):
            scores(0, tb)


        for i in range(n_heads):
            j = i - 1
            finishing = j >= 0
            last = i == n_heads - 1
            nxt = i + 3
            if nxt < n_heads:
                load_rows(nxt, 0)
                load_rows(nxt, 1)
            if i == 1:
                for pair in range(4):
                    load_mask(1, pair)
            if 2 <= i + 2 < n_heads:
                load_v(i + 2, 1)
                load_v(i + 2, 0)
            late = [tb for tb in range(TB) if tb not in early(j)] if finishing else []
            for step in range(max(TB, len(late) + REGROUP_BEHIND)):
                if PREFETCH <= step + SCORES_AHEAD < TB:
                    scores(i, step + SCORES_AHEAD)
                if i == 0 and step == 1:
                    keep_half(sca, 0, "q", 1)
                    keep_half(sca, 0, "k", 1)
                if i + 1 < n_heads:
                    if step == TURN_QK_STEP:
                        turn_all(i + 1, "q")
                    if step == TURN_QK_STEP + 1:
                        turn_all(i + 1, "k")
                        keep_turned(sca, i + 1, "q")
                    if step == TURN_QK_STEP + 2:
                        keep_turned(sca, i + 1, "k")
                for (h, g, n0, n1) in G_WORK(i).get(step, ()):
                    regroup_v_gpsimd(h, g, n0, n1)
                for tb in SCALAR_SCALES:
                    if finishing and step == max(tb - 2, 0):
                        nc.scalar.activation(
                            out=p_of(j, tb)[:, : (tb + 1) * P], in_=state[j]["r"][tb][:],
                            func=mybir.ActivationFunctionType.Copy, scale=state[j]["inverse"][tb],
                        )
                if step < len(late) and late[step] not in SCALAR_SCALES:
                    scale_rows(nc.gpsimd, j, late[step])
                if step < TB:
                    mask_scores(i, step)
                if 0 <= step - TURN_BEHIND < len(late):
                    turn_p(j, late[step - TURN_BEHIND])
                if 0 <= step - REGROUP_BEHIND < len(late):
                    tb = late[step - REGROUP_BEHIND]
                    regroup_p(vec if tb in V_REGROUPS(i) else sca, j, tb)
                for (h, g, n0, n1) in S_WORK(i).get(step, ()):
                    regroup_v(sca, h, g, n0, n1)
                if i == 0 and step == TM0:
                    pass
            for tb in early(i):
                turn_p(i, tb)
            if False:
                turn_mask(1, i - 2)
            if i + 1 < n_heads:
                for tb in range(PREFETCH):
                    scores(i + 1, tb)
            for tb in early(i):
                regroup_p(sca, i, tb)
            if i + 1 < n_heads and early(i + 1):
                early_sums(i + 1)
            if i == 0:
                join_row_sums(i)
                clip_row_sums()
                invert_row_sums(i)
                continue
            if i == 1:
                quantise_v(0, 0)
                quantise_v(0, 1)
            for tb in range(QUANTISED_FIRST):
                quantise_p(j, tb)
            join_row_sums(i)
            if last:
                clip_row_sums()
            for (h, g, n0, n1) in V_WORK(i):
                regroup_v(vec, h, g, n0, n1)
            for tb in range(QUANTISED_FIRST, TB):
                if last and tb == 4:
                    invert_row_sums(i)
                quantise_p(j, tb)
            if not last and early(i + 1):
                early_sums2(i + 1)
            quantise_v(i, 0)
            if not last:
                clip_row_sums()
            quantise_v(i, 1)
            if not last:
                invert_row_sums(i)
            for tb in range(TB + 1):
                if tb < TB:
                    multiply(j, tb)
                if tb > 0 and tb % 2 == 0:
                    store_pair(sca, j, tb - 1)

        j = n_heads - 1
        order = (0,1,2,3,4,5,6,7)
        n = len(order)
        for step in range(n + 6):
            if step < n:
                tb = order[step]
                if tb not in ():
                    scale_rows(nc.vector, j, tb)
            if 0 <= step - 1 < n and order[step - 1] not in ():
                turn_p(j, order[step - 1])
            if 0 <= step - 2 < n:
                tb = order[step - 2]
                if tb not in ():
                    regroup_p(vec if tb in (0,1,3,5) else sca, j, tb)
            if 0 <= step - 3 < n:
                quantise_p(j, order[step - 3])
            if 0 <= step - 4 < n:
                multiply(j, order[step - 4])
            if 0 <= step - 5 < n:
                tb = order[step - 5]
                store(vec if tb in (3, 5, 7) else sca, j, tb)
